import numpy as np
import ml_dtypes


def mxq(x, axis, fmt="e4m3"):
    dtype, down = {"e4m3": (ml_dtypes.float8_e4m3fn, 7), "e5m2": (ml_dtypes.float8_e5m2, 14)}[fmt]
    v = np.moveaxis(np.asarray(x, np.float32).astype(ml_dtypes.bfloat16).astype(np.float64), axis, -1)
    blocks = v.reshape(v.shape[:-1] + (-1, 32))
    amax = np.abs(blocks).max(-1, keepdims=True)
    byte = np.maximum(np.where(amax > 0, np.frexp(amax)[1] - 1 + 127, 0) - down, 1)
    scale = np.exp2(byte - 127.0)
    codes = (blocks / scale).astype(np.float32).astype(dtype).astype(np.float64)
    return np.moveaxis((codes * scale).reshape(v.shape), -1, axis)


WIDE = False


def mx_kscale(k):
    if not WIDE:
        return np.ones(k)
    levels = np.array([10, -10, 5, -5, 0])
    a = np.random.permutation(np.resize(levels, k // 512 * 4)).reshape(k // 512, 4)
    idx = np.arange(k)
    return np.exp2(a[idx // 512, idx % 128 // 32])


BF16 = ml_dtypes.bfloat16


def bf(x):
    return np.asarray(x, np.float32).astype(BF16)


def f64(x):
    return np.asarray(x).astype(np.float64)


E2M1 = np.array([0.0, 0.5, 1.0, 1.5, 2.0, 3.0, 4.0, 6.0, -0.0, -0.5, -1.0, -1.5, -2.0, -3.0, -4.0, -6.0])


def pack_weight(w, fmt):
    k, n = w.shape
    w = f64(bf(w)).reshape(k // 32, 32, n)
    amax = np.abs(w).max(1)
    if fmt == "e4m3":
        byte = np.frexp(amax)[1] - 1 + 127 - 7
    else:
        mant, ex = np.frexp(amax / 6.0)
        byte = np.where(mant > 0.5, ex, ex - 1) + 127
    byte = np.clip(np.where(amax > 0, byte, 1), 1, 254)
    scaled = (w * np.exp2(127.0 - byte)[:, None, :]).reshape(k, n).astype(np.float32)
    by_word = np.ascontiguousarray(scaled.reshape(k // 512, 128, 4, n).transpose(0, 1, 3, 2))
    if fmt == "e4m3":
        words = by_word.astype(ml_dtypes.float8_e4m3fn).view(np.uint8)
    else:
        c = by_word.astype(ml_dtypes.float4_e2m1fn).view(np.uint8) & 0xF
        words = c[..., 0::2] | (c[..., 1::2] << 4)
    return np.ascontiguousarray(words), np.ascontiguousarray(byte.astype(np.uint8).reshape(k // 512, 16, n))


def unpack_weight(words, scales, fmt):
    g, p, n, _ = words.shape
    if fmt == "e4m3":
        vals = np.ascontiguousarray(words).view(ml_dtypes.float8_e4m3fn).astype(np.float64)
    else:
        nib = np.empty((g, p, n, 4), np.uint8)
        nib[..., 0::2] = words & 0xF
        nib[..., 1::2] = words >> 4
        vals = E2M1[nib]
    vals = vals * np.repeat(np.exp2(scales.astype(np.float64) - 127.0), 8, axis=1)[..., None]
    return vals.transpose(0, 1, 3, 2).reshape(g * 512, n)


B, N, D = 512, 17, 512
LN_EPS = 1e-5
LEAKY_SLOPE = 0.01
FMT = "e4m3"


def setup_inputs():
    s = mx_kscale(D)
    s = s / s.max()
    h = bf(np.random.standard_normal((B, N, D)) * 0.5 * s)
    W_l = np.random.standard_normal((D, D)) * 2.0 / np.sqrt(D) / s[None, :]
    W_l_words, W_l_scales = pack_weight(np.ascontiguousarray(W_l.T), FMT)
    b_l = bf(np.random.standard_normal(D) * 0.1)
    W_r = np.random.standard_normal((D, D)) * 1.0 / np.sqrt(D) / s[None, :]
    W_r_words, W_r_scales = pack_weight(np.ascontiguousarray(W_r.T), FMT)
    ln_g = bf(1.0 + 0.1 * np.random.standard_normal(D))
    ln_b = bf(-0.4 + 0.2 * np.random.standard_normal(D))
    return {"h": h,
            "W_l_words": W_l_words,
            "W_l_scales": W_l_scales,
            "b_l": b_l,
            "W_r_words": W_r_words,
            "W_r_scales": W_r_scales,
            "ln_g": ln_g,
            "ln_b": ln_b}


def reference(h, W_l_words, W_l_scales, b_l, W_r_words, W_r_scales, ln_g, ln_b):
    h = f64(h)
    n = h.shape[1]
    mean_neigh = (np.sum(h, axis=1, keepdims=True) - h) / (n - 1)
    c = ((mxq(mean_neigh, 2, "e4m3") @ unpack_weight(W_l_words, W_l_scales, FMT)) + f64(b_l)
         + (mxq(h, 2, "e4m3") @ unpack_weight(W_r_words, W_r_scales, FMT)))
    mu = np.mean(c, axis=-1, keepdims=True)
    var = np.mean(np.square(c - mu), axis=-1, keepdims=True)
    y = (c - mu) * (1.0 / np.sqrt(var + LN_EPS)) * f64(ln_g) + f64(ln_b)
    a = np.where(y > 0, y, LEAKY_SLOPE * y)
    return a + h

@@ -1,0 +1,321 @@
+from contextlib import ExitStack
+
+import concourse.mybir as mybir
+from concourse.masks import make_identity
+
+F32 = mybir.dt.float32
+BF16 = mybir.dt.bfloat16
+I32 = mybir.dt.int32
+U32 = mybir.dt.uint32
+U8 = mybir.dt.uint8
+FP8X4 = mybir.dt.float8_e4m3fn_x4
+ALU = mybir.AluOpType
+ACT = mybir.ActivationFunctionType
+
+P = 128
+PACK = 4
+GRAPHS = 512
+NODES = 17
+D = 512
+FEATURE_BLOCKS = D // P
+ROWS = GRAPHS * NODES
+ROW_TILES = ROWS // P
+SPAN_TILES = NODES
+SPAN_ROWS = SPAN_TILES * P
+CHUNK_GRAPHS = 32
+CHUNK_ROWS = CHUNK_GRAPHS * NODES
+CHUNKS_PER_SPAN = SPAN_ROWS // CHUNK_ROWS
+CHUNKS = ROWS // CHUNK_ROWS
+CHUNK_TILES = 5
+GROUP = 4
+GROUPS = ROW_TILES // GROUP
+LN_EPS = 1e-5
+LEAKY_SLOPE = 0.01
+
+FLOPS = 2 * 2 * ROWS * D * D
+
+
+def load_weight(nc, pool, words_dram, scales_dram, label):
+    words = pool.tile([P, D], U32, name=label + "_words", align_bytes=64)
+    nc.sync.dma_start(
+        out=words[:].bitcast(I32),
+        in_=words_dram[0].rearrange("p n t -> p (n t)").bitcast(I32),
+    )
+    plane = pool.tile([P, D], U8, name=label + "_plane", align_bytes=64)
+    nc.vector.memset(plane[:].bitcast(I32), 0)
+    scale_rows = scales_dram[0].bitcast(I32)
+    for quadrant in range(4):
+        nc.sync.dma_start(
+            out=plane[32 * quadrant : 32 * quadrant + 4, :].bitcast(I32),
+            in_=scale_rows[4 * quadrant : 4 * quadrant + 4, :],
+        )
+    return words, plane
+
+
+def tile_gnnnicheencoder_pa_t_kernel(
+    tc, h, W_l_words, W_l_scales, b_l, W_r_words, W_r_scales, ln_g, ln_b, out
+):
+    nc = tc.nc
+    h_flat = h.flatten_outer_dims()
+    out_flat = out.flatten_outer_dims()
+
+    with ExitStack() as ctx:
+        consts = ctx.enter_context(tc.tile_pool(name="consts", bufs=1))
+        h_pool = ctx.enter_context(tc.tile_pool(name="h_pool", bufs=2))
+        grouped_pool = ctx.enter_context(tc.tile_pool(name="grouped_pool", bufs=2))
+        mean_pool = ctx.enter_context(tc.tile_pool(name="mean_pool", bufs=1))
+        mx_pool = ctx.enter_context(tc.tile_pool(name="mx_pool", bufs=2))
+        work = ctx.enter_context(tc.tile_pool(name="work", bufs=2))
+        stats = ctx.enter_context(tc.tile_pool(name="stats", bufs=3))
+        turn_psum = ctx.enter_context(tc.psum_pool(name="turn_psum", bufs=2))
+        acc_psum = ctx.enter_context(tc.psum_pool(name="acc_psum", bufs=2))
+        zt_psum = ctx.enter_context(tc.psum_pool(name="zt_psum", bufs=2))
+        back_psum = ctx.enter_context(tc.psum_pool(name="back_psum", bufs=2))
+
+        ident = consts.tile([P, P], F32, name="ident")
+        make_identity(nc, ident[:])
+
+        row_in_graph = consts.tile([P, CHUNKS_PER_SPAN, CHUNK_TILES, CHUNK_GRAPHS], I32, name="row_in_graph")
+        nc.gpsimd.iota(
+            row_in_graph[:],
+            pattern=[[(CHUNK_ROWS // P) * P - CHUNK_ROWS, CHUNKS_PER_SPAN], [P, CHUNK_TILES], [-NODES, CHUNK_GRAPHS]],
+            base=0,
+            channel_multiplier=1,
+        )
+        not_before = consts.tile([P, CHUNKS_PER_SPAN, CHUNK_TILES, CHUNK_GRAPHS], BF16, name="not_before")
+        nc.vector.tensor_single_scalar(
+            out=not_before[:].rearrange("p q i g -> p (q i g)"),
+            in_=row_in_graph[:].rearrange("p q i g -> p (q i g)"),
+            scalar=0.0,
+            op=ALU.is_ge,
+        )
+        member = consts.tile([P, CHUNKS_PER_SPAN, CHUNK_TILES, CHUNK_GRAPHS], BF16, name="member")
+        nc.vector.scalar_tensor_tensor(
+            out=member[:].rearrange("p q i g -> p (q i g)"),
+            in0=row_in_graph[:].rearrange("p q i g -> p (q i g)"),
+            scalar=float(NODES - 1),
+            in1=not_before[:].rearrange("p q i g -> p (q i g)"),
+            op0=ALU.is_le,
+            op1=ALU.mult,
+        )
+
+        eps_col = consts.tile([P, 1], F32, name="eps_col")
+        nc.vector.memset(eps_col[:], LN_EPS)
+
+        spans = {}
+
+        def open_span(s):
+            spans[s] = {
+                "h_rows": h_pool.tile([P, SPAN_TILES, D], BF16, name="h_rows"),
+                "h_grouped": grouped_pool.tile([P, SPAN_ROWS, PACK], BF16, name="h_grouped", align_bytes=64),
+                "m_grouped": mean_pool.tile([P, SPAN_ROWS, PACK], BF16, name="m_grouped", align_bytes=64),
+                "h_words": mx_pool.tile([P, SPAN_ROWS], U32, name="h_words", align_bytes=64),
+                "h_plane": mx_pool.tile([P, SPAN_ROWS], U8, name="h_plane", align_bytes=64),
+                "m_words": mx_pool.tile([P, SPAN_ROWS], U32, name="m_words", align_bytes=64),
+                "m_plane": mx_pool.tile([P, SPAN_ROWS], U8, name="m_plane", align_bytes=64),
+            }
+
+        def quantise_tile(span, kind, T):
+            rows = slice(P * T, P * (T + 1))
+            nc.vector.quantize_mx(
+                out=span[kind + "_words"][:, rows].bitcast(FP8X4),
+                scales=span[kind + "_plane"][:, rows],
+                in_=span[kind + "_grouped"][:, rows, :].rearrange("p r t -> p (r t)"),
+            )
+
+        def prepare_chunk(chunk):
+            s, q = divmod(chunk, CHUNKS_PER_SPAN)
+            if q == 0:
+                open_span(s)
+            span = spans[s]
+            h_rows = span["h_rows"]
+            first_row = CHUNK_ROWS * q
+            last_row = first_row + CHUNK_ROWS
+            first_tile = first_row // P
+            first_new = -(-first_row // P)
+            end_new = -(-last_row // P)
+            end_full = last_row // P
+
+            nc.sync.dma_start(
+                out=h_rows[:, first_new:end_new, :],
+                in_=h_flat[SPAN_ROWS * s + P * first_new : SPAN_ROWS * s + P * end_new, :].rearrange(
+                    "(T p) f -> p T f", p=P
+                ),
+            )
+
+            for T in range(first_new, end_new):
+                pairs = h_rows[:, T, :].bitcast(F32)
+                turned = turn_psum.tile([P, 2, P], F32, name="turned", tag="turn")
+                for u in range(2):
+                    nc.tensor.transpose(turned[:, u, :], pairs[:, u : D // 2 : 2], ident[:])
+                rows = slice(P * T, P * (T + 1))
+                nc.scalar.copy(
+                    out=span["h_grouped"][:, rows, :]
+                    .rearrange("p r t -> p (r t)")
+                    .bitcast(F32)
+                    .rearrange("p (r u) -> p r u", u=2),
+                    in_=turned[:].rearrange("p u r -> p r u"),
+                )
+                quantise_tile(span, "h", T)
+
+            sums_ps = turn_psum.tile([P, PACK, CHUNK_GRAPHS], F32, name="sums_ps", tag="turn")
+            for t in range(PACK):
+                for i in range(CHUNK_TILES):
+                    nc.tensor.matmul(
+                        out=sums_ps[:, t, :],
+                        lhsT=h_rows[:, first_tile + i, t:D:PACK],
+                        rhs=member[:, q, i, :],
+                        start=(i == 0),
+                        stop=(i == CHUNK_TILES - 1),
+                    )
+            sums = stats.tile([P, CHUNK_GRAPHS, PACK], F32, name="sums")
+            nc.scalar.copy(out=sums[:], in_=sums_ps[:].rearrange("p t g -> p g t"))
+
+            chunk_rows = slice(first_row, last_row)
+            m_chunk = span["m_grouped"][:, chunk_rows, :]
+            nc.vector.tensor_tensor(
+                out=m_chunk.rearrange("p (g n) t -> p g n t", n=NODES),
+                in0=sums[:].unsqueeze(2).to_broadcast([P, CHUNK_GRAPHS, NODES, PACK]),
+                in1=span["h_grouped"][:, chunk_rows, :].rearrange("p (g n) t -> p g n t", n=NODES),
+                op=ALU.subtract,
+            )
+            nc.vector.tensor_scalar_mul(
+                out=m_chunk.rearrange("p r t -> p (r t)"),
+                in0=m_chunk.rearrange("p r t -> p (r t)"),
+                scalar1=1.0 / (NODES - 1),
+            )
+            for T in range(first_tile, end_full):
+                quantise_tile(span, "m", T)
+
+        groups = {}
+
+        def multiply_and_normalise(group):
+            c = work.tile([P, GROUP, D], F32, name="c")
+            row_sum = stats.tile([P, GROUP], F32, name="row_sum")
+            for i in range(GROUP):
+                s, T = divmod(GROUP * group + i, SPAN_TILES)
+                span = spans[s]
+                rows = slice(P * T, P * (T + 1))
+                acc = acc_psum.tile([P, D], F32, name="acc")
+                nc.tensor.matmul_mx(
+                    out=acc[:],
+                    lhsT=span["m_words"][:, rows].bitcast(FP8X4),
+                    lhsT_scale=span["m_plane"][:, rows],
+                    rhs=wl_words[:].bitcast(FP8X4),
+                    rhs_scale=wl_plane[:],
+                    start=True,
+                    stop=False,
+                )
+                nc.tensor.matmul_mx(
+                    out=acc[:],
+                    lhsT=span["h_words"][:, rows].bitcast(FP8X4),
+                    lhsT_scale=span["h_plane"][:, rows],
+                    rhs=wr_words[:].bitcast(FP8X4),
+                    rhs_scale=wr_plane[:],
+                    start=False,
+                    stop=True,
+                )
+                nc.vector.scalar_tensor_tensor(
+                    out=c[:, i, :],
+                    in0=acc[:],
+                    scalar=1.0,
+                    in1=bias_rows[:],
+                    op0=ALU.mult,
+                    op1=ALU.add,
+                    accum_out=row_sum[:, i : i + 1],
+                )
+            neg_mean = stats.tile([P, GROUP], F32, name="neg_mean")
+            nc.vector.tensor_scalar_mul(out=neg_mean[:], in0=row_sum[:], scalar1=-1.0 / D)
+            sq_sum = stats.tile([P, GROUP], F32, name="sq_sum")
+            for i in range(GROUP):
+                squares = work.tile([P, D], F32, name="squares")
+                nc.scalar.activation(
+                    out=squares[:],
+                    in_=c[:, i, :],
+                    func=ACT.Square,
+                    bias=neg_mean[:, i : i + 1],
+                    scale=1.0,
+                    accum_out=sq_sum[:, i : i + 1],
+                )
+            std = stats.tile([P, GROUP], F32, name="std")
+            nc.scalar.activation(out=std[:], in_=sq_sum[:], func=ACT.Sqrt, bias=eps_col[:], scale=1.0 / D)
+            rstd = stats.tile([P, GROUP], F32, name="rstd")
+            nc.vector.reciprocal(out=rstd[:], in_=std[:])
+            neg_mean_rstd = stats.tile([P, GROUP], F32, name="neg_mean_rstd")
+            nc.vector.tensor_mul(out=neg_mean_rstd[:], in0=neg_mean[:], in1=rstd[:])
+            z = work.tile([P, GROUP, D], F32, name="z")
+            for i in range(GROUP):
+                nc.scalar.activation(
+                    out=z[:, i, :],
+                    in_=c[:, i, :],
+                    func=ACT.Identity,
+                    bias=neg_mean_rstd[:, i : i + 1],
+                    scale=rstd[:, i : i + 1],
+                )
+            groups[group] = z
+
+        def finish(group):
+            z = groups[group]
+            result = work.tile([P, GROUP, D], F32, name="result")
+            for i in range(GROUP):
+                s, T = divmod(GROUP * group + i, SPAN_TILES)
+                z_turned = zt_psum.tile([P, FEATURE_BLOCKS, P], F32, name="z_turned")
+                for j in range(FEATURE_BLOCKS):
+                    nc.tensor.transpose(z_turned[:, j, :], z[:, i, P * j : P * (j + 1)], ident[:])
+                y_turned = work.tile([P, FEATURE_BLOCKS, P], F32, name="y_turned")
+                for j in range(FEATURE_BLOCKS):
+                    nc.scalar.activation(
+                        out=y_turned[:, j, :],
+                        in_=z_turned[:, j, :],
+                        func=ACT.Identity,
+                        bias=affine_cols[:, FEATURE_BLOCKS + j : FEATURE_BLOCKS + j + 1],
+                        scale=affine_cols[:, j : j + 1],
+                    )
+                a_turned = work.tile([P, FEATURE_BLOCKS, P], F32, name="a_turned")
+                nc.vector.scalar_tensor_tensor(
+                    out=a_turned[:].rearrange("p j r -> p (j r)"),
+                    in0=y_turned[:].rearrange("p j r -> p (j r)"),
+                    scalar=LEAKY_SLOPE,
+                    in1=y_turned[:].rearrange("p j r -> p (j r)"),
+                    op0=ALU.mult,
+                    op1=ALU.max,
+                )
+                a_rows = back_psum.tile([P, D], F32, name="a_rows")
+                for j in range(FEATURE_BLOCKS):
+                    nc.tensor.transpose(a_rows[:, P * j : P * (j + 1)], a_turned[:, j, :], ident[:])
+                nc.vector.tensor_tensor(
+                    out=result[:, i, :], in0=a_rows[:], in1=spans[s]["h_rows"][:, T, :], op=ALU.add
+                )
+            first = GROUP * P * group
+            nc.sync.dma_start(
+                out=out_flat[first : first + GROUP * P, :].rearrange("(i p) f -> p i f", p=P),
+                in_=result[:],
+            )
+
+        prepare_chunk(0)
+
+        wl_words, wl_plane = load_weight(nc, consts, W_l_words, W_l_scales, "wl")
+        wr_words, wr_plane = load_weight(nc, consts, W_r_words, W_r_scales, "wr")
+        bias_rows = consts.tile([P, D], BF16, name="bias_rows")
+        nc.scalar.dma_start(out=bias_rows[:], in_=b_l.partition_broadcast(P))
+
+        affine_rows = consts.tile([P, P], BF16, name="affine_rows")
+        nc.vector.memset(affine_rows[:], 0.0)
+        nc.scalar.dma_start(out=affine_rows[0:FEATURE_BLOCKS, :], in_=ln_g.rearrange("(j p) -> j p", p=P))
+        nc.scalar.dma_start(
+            out=affine_rows[FEATURE_BLOCKS : 2 * FEATURE_BLOCKS, :], in_=ln_b.rearrange("(j p) -> j p", p=P)
+        )
+        affine_rows_f32 = consts.tile([P, P], F32, name="affine_rows_f32")
+        nc.vector.tensor_copy(out=affine_rows_f32[:], in_=affine_rows[:])
+        affine_ps = turn_psum.tile([P, P], F32, name="affine_ps", tag="turn")
+        nc.tensor.transpose(affine_ps[:], affine_rows_f32[:], ident[:])
+        affine_cols = consts.tile([P, 2 * FEATURE_BLOCKS], F32, name="affine_cols")
+        nc.vector.tensor_copy(out=affine_cols[:], in_=affine_ps[:, 0 : 2 * FEATURE_BLOCKS])
+
+        for step in range(1, GROUPS + 2):
+            if step < CHUNKS:
+                prepare_chunk(step)
+            if step - 1 < GROUPS:
+                multiply_and_normalise(step - 1)
+            if step >= 2:
+                finish(step - 2)

@@ -173,7 +173,7 @@ def tile_gnnnicheencoder_pa_t_kernel(
 
             chunk_rows = slice(first_row, last_row)
             m_chunk = span["m_grouped"][:, chunk_rows, :]
-            nc.vector.tensor_tensor(
+            nc.gpsimd.tensor_tensor(
                 out=m_chunk.rearrange("p (g n) t -> p g n t", n=NODES),
                 in0=sums[:].unsqueeze(2).to_broadcast([P, CHUNK_GRAPHS, NODES, PACK]),
                 in1=span["h_grouped"][:, chunk_rows, :].rearrange("p (g n) t -> p g n t", n=NODES),

@@ -27,12 +27,35 @@ CHUNK_ROWS = CHUNK_GRAPHS * NODES
 CHUNKS_PER_SPAN = SPAN_ROWS // CHUNK_ROWS
 CHUNKS = ROWS // CHUNK_ROWS
 CHUNK_TILES = 5
-GROUP = 4
-GROUPS = ROW_TILES // GROUP
 LN_EPS = 1e-5
 LEAKY_SLOPE = 0.01
 
+LOAD_LEAD = 8
+TURN_H = 0
+COPY_H = TURN_H + 1
+QUANTISE_H = COPY_H + 1
+SUBTRACT = COPY_H + 1
+DIVIDE = SUBTRACT + 1
+QUANTISE_M = (CHUNK_TILES - 1) + DIVIDE + 1
+MULTIPLY = QUANTISE_M + 1
+ADD_BIAS = MULTIPLY + 1
+VARIANCE = ADD_BIAS + 1
+INVERT_STD = VARIANCE + 1
+NORMALISE = INVERT_STD + 1
+TURN_Z = NORMALISE + 1
+AFFINE = TURN_Z + 1
+LEAKY = AFFINE + 1
+TURN_BACK = LEAKY + 1
+RESIDUAL = TURN_BACK + 1
+
 FLOPS = 2 * 2 * ROWS * D * D
+
+
+def chunk_tiles(chunk):
+    span, q = divmod(chunk, CHUNKS_PER_SPAN)
+    first_row = CHUNK_ROWS * q
+    base = SPAN_TILES * span
+    return base + first_row // P, base - (-first_row // P), base - (-(first_row + CHUNK_ROWS) // P)
 
 
 def load_weight(nc, pool, words_dram, scales_dram, label):
@@ -60,244 +83,46 @@ def tile_gnnnicheencoder_pa_t_kernel(
     out_flat = out.flatten_outer_dims()
 
     with ExitStack() as ctx:
+        ctx.enter_context(tc.manual_schedule())
         consts = ctx.enter_context(tc.tile_pool(name="consts", bufs=1))
-        h_pool = ctx.enter_context(tc.tile_pool(name="h_pool", bufs=2))
-        grouped_pool = ctx.enter_context(tc.tile_pool(name="grouped_pool", bufs=2))
-        mean_pool = ctx.enter_context(tc.tile_pool(name="mean_pool", bufs=1))
-        mx_pool = ctx.enter_context(tc.tile_pool(name="mx_pool", bufs=2))
-        work = ctx.enter_context(tc.tile_pool(name="work", bufs=2))
-        stats = ctx.enter_context(tc.tile_pool(name="stats", bufs=3))
+        h_pool = ctx.enter_context(tc.tile_pool(name="h_pool", bufs=3))
+        span_pool = ctx.enter_context(tc.tile_pool(name="span_pool", bufs=2))
+        c_pool = ctx.enter_context(tc.tile_pool(name="c_pool", bufs=5))
+        work = ctx.enter_context(tc.tile_pool(name="work", bufs=3))
+        stats = ctx.enter_context(tc.tile_pool(name="stats", bufs=6))
         turn_psum = ctx.enter_context(tc.psum_pool(name="turn_psum", bufs=2))
         acc_psum = ctx.enter_context(tc.psum_pool(name="acc_psum", bufs=2))
         zt_psum = ctx.enter_context(tc.psum_pool(name="zt_psum", bufs=2))
         back_psum = ctx.enter_context(tc.psum_pool(name="back_psum", bufs=2))
 
-        ident = consts.tile([P, P], F32, name="ident")
-        make_identity(nc, ident[:])
+        h_rows = {}
+        h_grouped = {}
+        m_grouped = {}
+        words = {}
+        planes = {}
+        sums = {}
+        live = {}
 
-        row_in_graph = consts.tile([P, CHUNKS_PER_SPAN, CHUNK_TILES, CHUNK_GRAPHS], I32, name="row_in_graph")
-        nc.gpsimd.iota(
-            row_in_graph[:],
-            pattern=[[(CHUNK_ROWS // P) * P - CHUNK_ROWS, CHUNKS_PER_SPAN], [P, CHUNK_TILES], [-NODES, CHUNK_GRAPHS]],
-            base=0,
-            channel_multiplier=1,
-        )
-        not_before = consts.tile([P, CHUNKS_PER_SPAN, CHUNK_TILES, CHUNK_GRAPHS], BF16, name="not_before")
-        nc.vector.tensor_single_scalar(
-            out=not_before[:].rearrange("p q i g -> p (q i g)"),
-            in_=row_in_graph[:].rearrange("p q i g -> p (q i g)"),
-            scalar=0.0,
-            op=ALU.is_ge,
-        )
-        member = consts.tile([P, CHUNKS_PER_SPAN, CHUNK_TILES, CHUNK_GRAPHS], BF16, name="member")
-        nc.vector.scalar_tensor_tensor(
-            out=member[:].rearrange("p q i g -> p (q i g)"),
-            in0=row_in_graph[:].rearrange("p q i g -> p (q i g)"),
-            scalar=float(NODES - 1),
-            in1=not_before[:].rearrange("p q i g -> p (q i g)"),
-            op0=ALU.is_le,
-            op1=ALU.mult,
-        )
-
-        eps_col = consts.tile([P, 1], F32, name="eps_col")
-        nc.vector.memset(eps_col[:], LN_EPS)
-
-        spans = {}
-
-        def open_span(s):
-            spans[s] = {
-                "h_rows": h_pool.tile([P, SPAN_TILES, D], BF16, name="h_rows"),
-                "h_grouped": grouped_pool.tile([P, SPAN_ROWS, PACK], BF16, name="h_grouped", align_bytes=64),
-                "m_grouped": mean_pool.tile([P, SPAN_ROWS, PACK], BF16, name="m_grouped", align_bytes=64),
-                "h_words": mx_pool.tile([P, SPAN_ROWS], U32, name="h_words", align_bytes=64),
-                "h_plane": mx_pool.tile([P, SPAN_ROWS], U8, name="h_plane", align_bytes=64),
-                "m_words": mx_pool.tile([P, SPAN_ROWS], U32, name="m_words", align_bytes=64),
-                "m_plane": mx_pool.tile([P, SPAN_ROWS], U8, name="m_plane", align_bytes=64),
-            }
-
-        def quantise_tile(span, kind, T):
-            rows = slice(P * T, P * (T + 1))
-            nc.vector.quantize_mx(
-                out=span[kind + "_words"][:, rows].bitcast(FP8X4),
-                scales=span[kind + "_plane"][:, rows],
-                in_=span[kind + "_grouped"][:, rows, :].rearrange("p r t -> p (r t)"),
-            )
-
-        def prepare_chunk(chunk):
-            s, q = divmod(chunk, CHUNKS_PER_SPAN)
-            if q == 0:
-                open_span(s)
-            span = spans[s]
-            h_rows = span["h_rows"]
-            first_row = CHUNK_ROWS * q
-            last_row = first_row + CHUNK_ROWS
-            first_tile = first_row // P
-            first_new = -(-first_row // P)
-            end_new = -(-last_row // P)
-            end_full = last_row // P
-
+        def load_chunk(chunk):
+            first, first_new, end = chunk_tiles(chunk)
+            span = first // SPAN_TILES
+            if chunk % CHUNKS_PER_SPAN == 0:
+                h_rows[span] = h_pool.tile([P, SPAN_TILES, D], BF16, name="h_rows")
             nc.sync.dma_start(
-                out=h_rows[:, first_new:end_new, :],
-                in_=h_flat[SPAN_ROWS * s + P * first_new : SPAN_ROWS * s + P * end_new, :].rearrange(
-                    "(T p) f -> p T f", p=P
-                ),
+                out=h_rows[span][:, first_new - SPAN_TILES * span : end - SPAN_TILES * span, :],
+                in_=h_flat[P * first_new : P * end, :].rearrange("(T p) f -> p T f", p=P),
             )
 
-            for T in range(first_new, end_new):
-                pairs = h_rows[:, T, :].bitcast(F32)
-                turned = turn_psum.tile([P, 2, P], F32, name="turned", tag="turn")
-                for u in range(2):
-                    nc.tensor.transpose(turned[:, u, :], pairs[:, u : D // 2 : 2], ident[:])
-                rows = slice(P * T, P * (T + 1))
-                nc.scalar.copy(
-                    out=span["h_grouped"][:, rows, :]
-                    .rearrange("p r t -> p (r t)")
-                    .bitcast(F32)
-                    .rearrange("p (r u) -> p r u", u=2),
-                    in_=turned[:].rearrange("p u r -> p r u"),
-                )
-                quantise_tile(span, "h", T)
-
-            sums_ps = turn_psum.tile([P, PACK, CHUNK_GRAPHS], F32, name="sums_ps", tag="turn")
-            for t in range(PACK):
-                for i in range(CHUNK_TILES):
-                    nc.tensor.matmul(
-                        out=sums_ps[:, t, :],
-                        lhsT=h_rows[:, first_tile + i, t:D:PACK],
-                        rhs=member[:, q, i, :],
-                        start=(i == 0),
-                        stop=(i == CHUNK_TILES - 1),
-                    )
-            sums = stats.tile([P, CHUNK_GRAPHS, PACK], F32, name="sums")
-            nc.scalar.copy(out=sums[:], in_=sums_ps[:].rearrange("p t g -> p g t"))
-
-            chunk_rows = slice(first_row, last_row)
-            m_chunk = span["m_grouped"][:, chunk_rows, :]
-            nc.gpsimd.tensor_tensor(
-                out=m_chunk.rearrange("p (g n) t -> p g n t", n=NODES),
-                in0=sums[:].unsqueeze(2).to_broadcast([P, CHUNK_GRAPHS, NODES, PACK]),
-                in1=span["h_grouped"][:, chunk_rows, :].rearrange("p (g n) t -> p g n t", n=NODES),
-                op=ALU.subtract,
-            )
-            nc.vector.tensor_scalar_mul(
-                out=m_chunk.rearrange("p r t -> p (r t)"),
-                in0=m_chunk.rearrange("p r t -> p (r t)"),
-                scalar1=1.0 / (NODES - 1),
-            )
-            for T in range(first_tile, end_full):
-                quantise_tile(span, "m", T)
-
-        groups = {}
-
-        def multiply_and_normalise(group):
-            c = work.tile([P, GROUP, D], F32, name="c")
-            row_sum = stats.tile([P, GROUP], F32, name="row_sum")
-            for i in range(GROUP):
-                s, T = divmod(GROUP * group + i, SPAN_TILES)
-                span = spans[s]
-                rows = slice(P * T, P * (T + 1))
-                acc = acc_psum.tile([P, D], F32, name="acc")
-                nc.tensor.matmul_mx(
-                    out=acc[:],
-                    lhsT=span["m_words"][:, rows].bitcast(FP8X4),
-                    lhsT_scale=span["m_plane"][:, rows],
-                    rhs=wl_words[:].bitcast(FP8X4),
-                    rhs_scale=wl_plane[:],
-                    start=True,
-                    stop=False,
-                )
-                nc.tensor.matmul_mx(
-                    out=acc[:],
-                    lhsT=span["h_words"][:, rows].bitcast(FP8X4),
-                    lhsT_scale=span["h_plane"][:, rows],
-                    rhs=wr_words[:].bitcast(FP8X4),
-                    rhs_scale=wr_plane[:],
-                    start=False,
-                    stop=True,
-                )
-                nc.vector.scalar_tensor_tensor(
-                    out=c[:, i, :],
-                    in0=acc[:],
-                    scalar=1.0,
-                    in1=bias_rows[:],
-                    op0=ALU.mult,
-                    op1=ALU.add,
-                    accum_out=row_sum[:, i : i + 1],
-                )
-            neg_mean = stats.tile([P, GROUP], F32, name="neg_mean")
-            nc.vector.tensor_scalar_mul(out=neg_mean[:], in0=row_sum[:], scalar1=-1.0 / D)
-            sq_sum = stats.tile([P, GROUP], F32, name="sq_sum")
-            for i in range(GROUP):
-                squares = work.tile([P, D], F32, name="squares")
-                nc.scalar.activation(
-                    out=squares[:],
-                    in_=c[:, i, :],
-                    func=ACT.Square,
-                    bias=neg_mean[:, i : i + 1],
-                    scale=1.0,
-                    accum_out=sq_sum[:, i : i + 1],
-                )
-            std = stats.tile([P, GROUP], F32, name="std")
-            nc.scalar.activation(out=std[:], in_=sq_sum[:], func=ACT.Sqrt, bias=eps_col[:], scale=1.0 / D)
-            rstd = stats.tile([P, GROUP], F32, name="rstd")
-            nc.vector.reciprocal(out=rstd[:], in_=std[:])
-            neg_mean_rstd = stats.tile([P, GROUP], F32, name="neg_mean_rstd")
-            nc.vector.tensor_mul(out=neg_mean_rstd[:], in0=neg_mean[:], in1=rstd[:])
-            z = work.tile([P, GROUP, D], F32, name="z")
-            for i in range(GROUP):
-                nc.scalar.activation(
-                    out=z[:, i, :],
-                    in_=c[:, i, :],
-                    func=ACT.Identity,
-                    bias=neg_mean_rstd[:, i : i + 1],
-                    scale=rstd[:, i : i + 1],
-                )
-            groups[group] = z
-
-        def finish(group):
-            z = groups[group]
-            result = work.tile([P, GROUP, D], F32, name="result")
-            for i in range(GROUP):
-                s, T = divmod(GROUP * group + i, SPAN_TILES)
-                z_turned = zt_psum.tile([P, FEATURE_BLOCKS, P], F32, name="z_turned")
-                for j in range(FEATURE_BLOCKS):
-                    nc.tensor.transpose(z_turned[:, j, :], z[:, i, P * j : P * (j + 1)], ident[:])
-                y_turned = work.tile([P, FEATURE_BLOCKS, P], F32, name="y_turned")
-                for j in range(FEATURE_BLOCKS):
-                    nc.scalar.activation(
-                        out=y_turned[:, j, :],
-                        in_=z_turned[:, j, :],
-                        func=ACT.Identity,
-                        bias=affine_cols[:, FEATURE_BLOCKS + j : FEATURE_BLOCKS + j + 1],
-                        scale=affine_cols[:, j : j + 1],
-                    )
-                a_turned = work.tile([P, FEATURE_BLOCKS, P], F32, name="a_turned")
-                nc.vector.scalar_tensor_tensor(
-                    out=a_turned[:].rearrange("p j r -> p (j r)"),
-                    in0=y_turned[:].rearrange("p j r -> p (j r)"),
-                    scalar=LEAKY_SLOPE,
-                    in1=y_turned[:].rearrange("p j r -> p (j r)"),
-                    op0=ALU.mult,
-                    op1=ALU.max,
-                )
-                a_rows = back_psum.tile([P, D], F32, name="a_rows")
-                for j in range(FEATURE_BLOCKS):
-                    nc.tensor.transpose(a_rows[:, P * j : P * (j + 1)], a_turned[:, j, :], ident[:])
-                nc.vector.tensor_tensor(
-                    out=result[:, i, :], in0=a_rows[:], in1=spans[s]["h_rows"][:, T, :], op=ALU.add
-                )
-            first = GROUP * P * group
-            nc.sync.dma_start(
-                out=out_flat[first : first + GROUP * P, :].rearrange("(i p) f -> p i f", p=P),
-                in_=result[:],
-            )
-
-        prepare_chunk(0)
-
+        for chunk in range(CHUNKS):
+            if chunk_tiles(chunk)[1] < LOAD_LEAD:
+                load_chunk(chunk)
         wl_words, wl_plane = load_weight(nc, consts, W_l_words, W_l_scales, "wl")
         wr_words, wr_plane = load_weight(nc, consts, W_r_words, W_r_scales, "wr")
         bias_rows = consts.tile([P, D], BF16, name="bias_rows")
         nc.scalar.dma_start(out=bias_rows[:], in_=b_l.partition_broadcast(P))
+
+        ident = consts.tile([P, P], F32, name="ident")
+        make_identity(nc, ident[:])
 
         affine_rows = consts.tile([P, P], BF16, name="affine_rows")
         nc.vector.memset(affine_rows[:], 0.0)
@@ -307,15 +132,269 @@ def tile_gnnnicheencoder_pa_t_kernel(
         )
         affine_rows_f32 = consts.tile([P, P], F32, name="affine_rows_f32")
         nc.vector.tensor_copy(out=affine_rows_f32[:], in_=affine_rows[:])
-        affine_ps = turn_psum.tile([P, P], F32, name="affine_ps", tag="turn")
+        affine_ps = turn_psum.tile([P, P], F32, name="affine_ps", tag="turned")
         nc.tensor.transpose(affine_ps[:], affine_rows_f32[:], ident[:])
         affine_cols = consts.tile([P, 2 * FEATURE_BLOCKS], F32, name="affine_cols")
         nc.vector.tensor_copy(out=affine_cols[:], in_=affine_ps[:, 0 : 2 * FEATURE_BLOCKS])
 
-        for step in range(1, GROUPS + 2):
-            if step < CHUNKS:
-                prepare_chunk(step)
-            if step - 1 < GROUPS:
-                multiply_and_normalise(step - 1)
-            if step >= 2:
-                finish(step - 2)
+        member_shape = [P, CHUNKS_PER_SPAN, CHUNK_TILES, CHUNK_GRAPHS]
+        row_in_graph = consts.tile(member_shape, I32, name="row_in_graph")
+        nc.gpsimd.iota(
+            row_in_graph[:],
+            pattern=[[(CHUNK_ROWS // P) * P - CHUNK_ROWS, CHUNKS_PER_SPAN], [P, CHUNK_TILES], [-NODES, CHUNK_GRAPHS]],
+            base=0,
+            channel_multiplier=1,
+        )
+        not_before = consts.tile(member_shape, BF16, name="not_before")
+        nc.vector.tensor_single_scalar(
+            out=not_before[:].rearrange("p q i g -> p (q i g)"),
+            in_=row_in_graph[:].rearrange("p q i g -> p (q i g)"),
+            scalar=0.0,
+            op=ALU.is_ge,
+        )
+        member = consts.tile(member_shape, BF16, name="member")
+        nc.vector.scalar_tensor_tensor(
+            out=member[:].rearrange("p q i g -> p (q i g)"),
+            in0=row_in_graph[:].rearrange("p q i g -> p (q i g)"),
+            scalar=float(NODES - 1),
+            in1=not_before[:].rearrange("p q i g -> p (q i g)"),
+            op0=ALU.is_le,
+            op1=ALU.mult,
+        )
+        eps_col = consts.tile([P, 1], F32, name="eps_col")
+        nc.vector.memset(eps_col[:], LN_EPS)
+
+        def turn_h(x):
+            span, T = divmod(x, SPAN_TILES)
+            turned = turn_psum.tile([P, 2 * P + CHUNK_GRAPHS], F32, name="turned")
+            live["turned", x] = turned
+            pairs = h_rows[span][:, T, :].bitcast(F32)
+            for u in range(2):
+                nc.tensor.transpose(turned[:, P * u : P * (u + 1)], pairs[:, u : D // 2 : 2], ident[:])
+            if T > 0:
+                q, t = divmod(T - 1, PACK)
+                for i in range(CHUNK_TILES):
+                    nc.tensor.matmul(
+                        out=turned[:, 2 * P :],
+                        lhsT=h_rows[span][:, (CHUNK_ROWS // P) * q + i, t:D:PACK],
+                        rhs=member[:, q, i, :],
+                        start=(i == 0),
+                        stop=(i == CHUNK_TILES - 1),
+                    )
+
+        def multiply(x):
+            span, T = divmod(x, SPAN_TILES)
+            rows = slice(P * T, P * (T + 1))
+            acc = acc_psum.tile([P, D], F32, name="acc")
+            live["acc", x] = acc
+            nc.tensor.matmul_mx(
+                out=acc[:],
+                lhsT=words["m", span][:, rows].bitcast(FP8X4),
+                lhsT_scale=planes["m", span][:, rows],
+                rhs=wl_words[:].bitcast(FP8X4),
+                rhs_scale=wl_plane[:],
+                start=True,
+                stop=False,
+            )
+            nc.tensor.matmul_mx(
+                out=acc[:],
+                lhsT=words["h", span][:, rows].bitcast(FP8X4),
+                lhsT_scale=planes["h", span][:, rows],
+                rhs=wr_words[:].bitcast(FP8X4),
+                rhs_scale=wr_plane[:],
+                start=False,
+                stop=True,
+            )
+
+        def turn_z(x):
+            z_turned = zt_psum.tile([P, FEATURE_BLOCKS, P], F32, name="z_turned")
+            live["z_turned", x] = z_turned
+            for j in range(FEATURE_BLOCKS):
+                nc.tensor.transpose(z_turned[:, j, :], live["z", x][:, P * j : P * (j + 1)], ident[:])
+
+        def turn_back(x):
+            a_rows = back_psum.tile([P, D], F32, name="a_rows")
+            live["a_rows", x] = a_rows
+            for j in range(FEATURE_BLOCKS):
+                nc.tensor.transpose(a_rows[:, P * j : P * (j + 1)], live["a_turned", x][:, j, :], ident[:])
+
+        def quantise(operand, grouped, x):
+            span, T = divmod(x, SPAN_TILES)
+            if T == 0:
+                words[operand, span] = span_pool.tile([P, SPAN_ROWS], U32, name=operand + "_words", align_bytes=64)
+                planes[operand, span] = span_pool.tile([P, SPAN_ROWS], U8, name=operand + "_plane", align_bytes=64)
+            rows = slice(P * T, P * (T + 1))
+            nc.vector.quantize_mx(
+                out=words[operand, span][:, rows].bitcast(FP8X4),
+                scales=planes[operand, span][:, rows],
+                in_=grouped[span][:, rows, :].rearrange("p r t -> p (r t)"),
+            )
+
+        def chunk_of(grouped, chunk):
+            span, q = divmod(chunk, CHUNKS_PER_SPAN)
+            return grouped[span][:, CHUNK_ROWS * q : CHUNK_ROWS * (q + 1), :]
+
+        def subtract(chunk):
+            span, q = divmod(chunk, CHUNKS_PER_SPAN)
+            if q == 0:
+                m_grouped[span] = span_pool.tile([P, SPAN_ROWS, PACK], BF16, name="m_grouped", align_bytes=64)
+            nc.vector.tensor_tensor(
+                out=chunk_of(m_grouped, chunk).rearrange("p (g n) t -> p g n t", n=NODES),
+                in0=sums[chunk][:]
+                .rearrange("p t g -> p g t")
+                .unsqueeze(2)
+                .to_broadcast([P, CHUNK_GRAPHS, NODES, PACK]),
+                in1=chunk_of(h_grouped, chunk).rearrange("p (g n) t -> p g n t", n=NODES),
+                op=ALU.subtract,
+            )
+
+        def divide(chunk):
+            m_chunk = chunk_of(m_grouped, chunk).rearrange("p r t -> p (r t)")
+            nc.vector.tensor_scalar_mul(out=m_chunk, in0=m_chunk, scalar1=1.0 / (NODES - 1))
+
+        def add_bias(x):
+            c = c_pool.tile([P, D], F32, name="c")
+            row_sum = stats.tile([P, 1], F32, name="row_sum")
+            live["c", x] = c
+            live["row_sum", x] = row_sum
+            nc.vector.scalar_tensor_tensor(
+                out=c[:],
+                in0=live["acc", x][:],
+                scalar=1.0,
+                in1=bias_rows[:],
+                op0=ALU.mult,
+                op1=ALU.add,
+                accum_out=row_sum[:],
+            )
+
+        def invert_std(x):
+            rstd = stats.tile([P, 1], F32, name="rstd")
+            live["rstd", x] = rstd
+            nc.vector.reciprocal(out=rstd[:], in_=live["std", x][:])
+
+        def leaky(x):
+            a_turned = work.tile([P, FEATURE_BLOCKS, P], F32, name="a_turned")
+            live["a_turned", x] = a_turned
+            y_flat = live["y_turned", x][:].rearrange("p j r -> p (j r)")
+            nc.vector.scalar_tensor_tensor(
+                out=a_turned[:].rearrange("p j r -> p (j r)"),
+                in0=y_flat,
+                scalar=LEAKY_SLOPE,
+                in1=y_flat,
+                op0=ALU.mult,
+                op1=ALU.max,
+            )
+
+        def residual_and_store(x):
+            span, T = divmod(x, SPAN_TILES)
+            result = work.tile([P, D], F32, name="result")
+            nc.vector.tensor_tensor(out=result[:], in0=live["a_rows", x][:], in1=h_rows[span][:, T, :], op=ALU.add)
+            nc.sync.dma_start(out=out_flat[P * x : P * (x + 1), :], in_=result[:])
+
+        def copy_h(x):
+            span, T = divmod(x, SPAN_TILES)
+            if T == 0:
+                h_grouped[span] = span_pool.tile([P, SPAN_ROWS, PACK], BF16, name="h_grouped", align_bytes=64)
+            turned = live["turned", x]
+            nc.scalar.copy(
+                out=h_grouped[span][:, P * T : P * (T + 1), :]
+                .rearrange("p r t -> p (r t)")
+                .bitcast(F32)
+                .rearrange("p (r u) -> p r u", u=2),
+                in_=turned[:, 0 : 2 * P].rearrange("p (u r) -> p r u", u=2),
+            )
+            if T > 0:
+                q, t = divmod(T - 1, PACK)
+                chunk = CHUNKS_PER_SPAN * span + q
+                if t == 0:
+                    sums[chunk] = work.tile([P, PACK, CHUNK_GRAPHS], F32, name="sums")
+                nc.scalar.copy(out=sums[chunk][:, t, :], in_=turned[:, 2 * P :])
+
+        def negate_mean(x):
+            neg_mean = stats.tile([P, 1], F32, name="neg_mean")
+            live["neg_mean", x] = neg_mean
+            nc.scalar.mul(out=neg_mean[:], in_=live["row_sum", x][:], mul=-1.0 / D)
+
+        def sum_squares(x):
+            squares = work.tile([P, D], F32, name="squares")
+            sq_sum = stats.tile([P, 1], F32, name="sq_sum")
+            live["sq_sum", x] = sq_sum
+            nc.scalar.activation(
+                out=squares[:],
+                in_=live["c", x][:],
+                func=ACT.Square,
+                bias=live["neg_mean", x][:],
+                scale=1.0,
+                accum_out=sq_sum[:],
+            )
+
+        def root(x):
+            std = stats.tile([P, 1], F32, name="std")
+            live["std", x] = std
+            nc.scalar.activation(out=std[:], in_=live["sq_sum", x][:], func=ACT.Sqrt, bias=eps_col[:], scale=1.0 / D)
+
+        def scale_mean(x):
+            neg_mean_rstd = stats.tile([P, 1], F32, name="neg_mean_rstd")
+            live["neg_mean_rstd", x] = neg_mean_rstd
+            nc.scalar.activation(
+                out=neg_mean_rstd[:], in_=live["neg_mean", x][:], func=ACT.Copy, scale=live["rstd", x][:]
+            )
+
+        def normalise(x):
+            z = work.tile([P, D], F32, name="z")
+            live["z", x] = z
+            nc.scalar.activation(
+                out=z[:],
+                in_=live["c", x][:],
+                func=ACT.Identity,
+                bias=live["neg_mean_rstd", x][:],
+                scale=live["rstd", x][:],
+            )
+
+        def affine(x):
+            y_turned = work.tile([P, FEATURE_BLOCKS, P], F32, name="y_turned")
+            live["y_turned", x] = y_turned
+            for j in range(FEATURE_BLOCKS):
+                nc.scalar.activation(
+                    out=y_turned[:, j, :],
+                    in_=live["z_turned", x][:, j, :],
+                    func=ACT.Identity,
+                    bias=affine_cols[:, FEATURE_BLOCKS + j : FEATURE_BLOCKS + j + 1],
+                    scale=affine_cols[:, j : j + 1],
+                )
+
+        chunk_by_first_new_tile = {chunk_tiles(chunk)[1]: chunk for chunk in range(CHUNKS)}
+        chunk_by_last_tile = {chunk_tiles(chunk)[2] - 1: chunk for chunk in range(CHUNKS)}
+
+        def for_tile(step, tick, lag):
+            if 0 <= tick - lag < ROW_TILES:
+                step(tick - lag)
+
+        def for_chunk(step, tick, lag):
+            chunk = chunk_by_last_tile.get(tick - lag)
+            if chunk is not None:
+                step(chunk)
+
+        for tick in range(ROW_TILES + RESIDUAL):
+            chunk = chunk_by_first_new_tile.get(tick + LOAD_LEAD)
+            if chunk is not None:
+                load_chunk(chunk)
+            for_tile(turn_h, tick, TURN_H)
+            for_tile(turn_back, tick, TURN_BACK)
+            for_tile(multiply, tick, MULTIPLY)
+            for_tile(turn_z, tick, TURN_Z)
+            for_tile(residual_and_store, tick, RESIDUAL)
+            for_tile(leaky, tick, LEAKY)
+            for_tile(add_bias, tick, ADD_BIAS)
+            for_tile(invert_std, tick, INVERT_STD)
+            for_tile(lambda x: quantise("h", h_grouped, x), tick, QUANTISE_H)
+            for_tile(lambda x: quantise("m", m_grouped, x), tick, QUANTISE_M)
+            for_chunk(divide, tick, DIVIDE)
+            for_chunk(subtract, tick, SUBTRACT)
+            for_tile(negate_mean, tick, VARIANCE)
+            for_tile(copy_h, tick, COPY_H)
+            for_tile(sum_squares, tick, VARIANCE)
+            for_tile(scale_mean, tick, NORMALISE)
+            for_tile(affine, tick, AFFINE)
+            for_tile(root, tick, VARIANCE)
+            for_tile(normalise, tick, NORMALISE)

@@ -27,6 +27,7 @@ CHUNK_ROWS = CHUNK_GRAPHS * NODES
 CHUNKS_PER_SPAN = SPAN_ROWS // CHUNK_ROWS
 CHUNKS = ROWS // CHUNK_ROWS
 CHUNK_TILES = 5
+LANE_HEAD = 3
 LN_EPS = 1e-5
 LEAKY_SLOPE = 0.01
 
@@ -171,11 +172,14 @@ def tile_gnnnicheencoder_pa_t_kernel(
             pairs = h_rows[span][:, T, :].bitcast(F32)
             for u in range(2):
                 nc.tensor.transpose(turned[:, P * u : P * (u + 1)], pairs[:, u : D // 2 : 2], ident[:])
+
+        def sum_lane(x, first_part, end_part):
+            span, T = divmod(x, SPAN_TILES)
             if T > 0:
                 q, t = divmod(T - 1, PACK)
-                for i in range(CHUNK_TILES):
+                for i in range(first_part, end_part):
                     nc.tensor.matmul(
-                        out=turned[:, 2 * P :],
+                        out=live["turned", x][:, 2 * P :],
                         lhsT=h_rows[span][:, (CHUNK_ROWS // P) * q + i, t:D:PACK],
                         rhs=member[:, q, i, :],
                         start=(i == 0),
@@ -381,7 +385,9 @@ def tile_gnnnicheencoder_pa_t_kernel(
                 load_chunk(chunk)
             for_tile(turn_h, tick, TURN_H)
             for_tile(turn_back, tick, TURN_BACK)
+            for_tile(lambda x: sum_lane(x, 0, LANE_HEAD), tick, TURN_H)
             for_tile(multiply, tick, MULTIPLY)
+            for_tile(lambda x: sum_lane(x, LANE_HEAD, CHUNK_TILES), tick, TURN_H)
             for_tile(turn_z, tick, TURN_Z)
             for_tile(residual_and_store, tick, RESIDUAL)
             for_tile(leaky, tick, LEAKY)

@@ -41,12 +41,10 @@ QUANTISE_M = (CHUNK_TILES - 1) + DIVIDE + 1
 MULTIPLY = QUANTISE_M + 1
 ADD_BIAS = MULTIPLY + 1
 VARIANCE = ADD_BIAS + 1
-INVERT_STD = VARIANCE + 1
-NORMALISE = INVERT_STD + 1
+NORMALISE = VARIANCE + 1
 TURN_Z = NORMALISE + 1
 AFFINE = TURN_Z + 1
-LEAKY = AFFINE + 1
-TURN_BACK = LEAKY + 1
+TURN_BACK = AFFINE + 1
 RESIDUAL = TURN_BACK + 1
 
 FLOPS = 2 * 2 * ROWS * D * D
@@ -137,6 +135,10 @@ def tile_gnnnicheencoder_pa_t_kernel(
         nc.tensor.transpose(affine_ps[:], affine_rows_f32[:], ident[:])
         affine_cols = consts.tile([P, 2 * FEATURE_BLOCKS], F32, name="affine_cols")
         nc.vector.tensor_copy(out=affine_cols[:], in_=affine_ps[:, 0 : 2 * FEATURE_BLOCKS])
+        relu_cols = consts.tile([P, 2 * FEATURE_BLOCKS], F32, name="relu_cols")
+        nc.vector.tensor_scalar_mul(out=relu_cols[:], in0=affine_cols[:], scalar1=1.0 - LEAKY_SLOPE)
+        line_cols = consts.tile([P, 2 * FEATURE_BLOCKS], F32, name="line_cols")
+        nc.vector.tensor_scalar_mul(out=line_cols[:], in0=affine_cols[:], scalar1=LEAKY_SLOPE)
 
         member_shape = [P, CHUNKS_PER_SPAN, CHUNK_TILES, CHUNK_GRAPHS]
         row_in_graph = consts.tile(member_shape, I32, name="row_in_graph")
@@ -220,7 +222,13 @@ def tile_gnnnicheencoder_pa_t_kernel(
             a_rows = back_psum.tile([P, D], F32, name="a_rows")
             live["a_rows", x] = a_rows
             for j in range(FEATURE_BLOCKS):
-                nc.tensor.transpose(a_rows[:, P * j : P * (j + 1)], live["a_turned", x][:, j, :], ident[:])
+                block = a_rows[:, P * j : P * (j + 1)]
+                nc.tensor.matmul(
+                    out=block, lhsT=live["relu_term", x][:, j, :], rhs=ident[:], is_transpose=True, start=True, stop=False
+                )
+                nc.tensor.matmul(
+                    out=block, lhsT=live["line_term", x][:, j, :], rhs=ident[:], is_transpose=True, start=False, stop=True
+                )
 
         def quantise(operand, grouped, x):
             span, T = divmod(x, SPAN_TILES)
@@ -271,22 +279,16 @@ def tile_gnnnicheencoder_pa_t_kernel(
                 accum_out=row_sum[:],
             )
 
-        def invert_std(x):
-            rstd = stats.tile([P, 1], F32, name="rstd")
-            live["rstd", x] = rstd
-            nc.vector.reciprocal(out=rstd[:], in_=live["std", x][:])
-
-        def leaky(x):
-            a_turned = work.tile([P, FEATURE_BLOCKS, P], F32, name="a_turned")
-            live["a_turned", x] = a_turned
-            y_flat = live["y_turned", x][:].rearrange("p j r -> p (j r)")
-            nc.vector.scalar_tensor_tensor(
-                out=a_turned[:].rearrange("p j r -> p (j r)"),
-                in0=y_flat,
-                scalar=LEAKY_SLOPE,
-                in1=y_flat,
-                op0=ALU.mult,
-                op1=ALU.max,
+        def normalise(x):
+            z = work.tile([P, D], F32, name="z")
+            live["z", x] = z
+            nc.vector.tensor_scalar(
+                out=z[:],
+                in0=live["c", x][:],
+                scalar1=live["neg_mean", x][:],
+                scalar2=live["rstd", x][:],
+                op0=ALU.add,
+                op1=ALU.mult,
             )
 
         def residual_and_store(x):
@@ -332,40 +334,27 @@ def tile_gnnnicheencoder_pa_t_kernel(
                 accum_out=sq_sum[:],
             )
 
-        def root(x):
-            std = stats.tile([P, 1], F32, name="std")
-            live["std", x] = std
-            nc.scalar.activation(out=std[:], in_=live["sq_sum", x][:], func=ACT.Sqrt, bias=eps_col[:], scale=1.0 / D)
-
-        def scale_mean(x):
-            neg_mean_rstd = stats.tile([P, 1], F32, name="neg_mean_rstd")
-            live["neg_mean_rstd", x] = neg_mean_rstd
+        def invert_std(x):
+            rstd = stats.tile([P, 1], F32, name="rstd")
+            live["rstd", x] = rstd
             nc.scalar.activation(
-                out=neg_mean_rstd[:], in_=live["neg_mean", x][:], func=ACT.Copy, scale=live["rstd", x][:]
+                out=rstd[:], in_=live["sq_sum", x][:], func=ACT.Abs_reciprocal_sqrt, bias=eps_col[:], scale=1.0 / D
             )
 
-        def normalise(x):
-            z = work.tile([P, D], F32, name="z")
-            live["z", x] = z
-            nc.scalar.activation(
-                out=z[:],
-                in_=live["c", x][:],
-                func=ACT.Identity,
-                bias=live["neg_mean_rstd", x][:],
-                scale=live["rstd", x][:],
-            )
-
-        def affine(x):
-            y_turned = work.tile([P, FEATURE_BLOCKS, P], F32, name="y_turned")
-            live["y_turned", x] = y_turned
-            for j in range(FEATURE_BLOCKS):
-                nc.scalar.activation(
-                    out=y_turned[:, j, :],
-                    in_=live["z_turned", x][:, j, :],
-                    func=ACT.Identity,
-                    bias=affine_cols[:, FEATURE_BLOCKS + j : FEATURE_BLOCKS + j + 1],
-                    scale=affine_cols[:, j : j + 1],
-                )
+        def affine_and_split(x):
+            relu_term = work.tile([P, FEATURE_BLOCKS, P], F32, name="relu_term")
+            line_term = work.tile([P, FEATURE_BLOCKS, P], F32, name="line_term")
+            live["relu_term", x] = relu_term
+            live["line_term", x] = line_term
+            for term, func, cols in ((relu_term, ACT.Relu, relu_cols), (line_term, ACT.Identity, line_cols)):
+                for j in range(FEATURE_BLOCKS):
+                    nc.scalar.activation(
+                        out=term[:, j, :],
+                        in_=live["z_turned", x][:, j, :],
+                        func=func,
+                        bias=cols[:, FEATURE_BLOCKS + j : FEATURE_BLOCKS + j + 1],
+                        scale=cols[:, j : j + 1],
+                    )
 
         chunk_by_first_new_tile = {chunk_tiles(chunk)[1]: chunk for chunk in range(CHUNKS)}
         chunk_by_last_tile = {chunk_tiles(chunk)[2] - 1: chunk for chunk in range(CHUNKS)}
@@ -390,9 +379,8 @@ def tile_gnnnicheencoder_pa_t_kernel(
             for_tile(lambda x: sum_lane(x, LANE_HEAD, CHUNK_TILES), tick, TURN_H)
             for_tile(turn_z, tick, TURN_Z)
             for_tile(residual_and_store, tick, RESIDUAL)
-            for_tile(leaky, tick, LEAKY)
             for_tile(add_bias, tick, ADD_BIAS)
-            for_tile(invert_std, tick, INVERT_STD)
+            for_tile(normalise, tick, NORMALISE)
             for_tile(lambda x: quantise("h", h_grouped, x), tick, QUANTISE_H)
             for_tile(lambda x: quantise("m", m_grouped, x), tick, QUANTISE_M)
             for_chunk(divide, tick, DIVIDE)
@@ -400,7 +388,5 @@ def tile_gnnnicheencoder_pa_t_kernel(
             for_tile(negate_mean, tick, VARIANCE)
             for_tile(copy_h, tick, COPY_H)
             for_tile(sum_squares, tick, VARIANCE)
-            for_tile(scale_mean, tick, NORMALISE)
-            for_tile(affine, tick, AFFINE)
-            for_tile(root, tick, VARIANCE)
-            for_tile(normalise, tick, NORMALISE)
+            for_tile(affine_and_split, tick, AFFINE)
+            for_tile(invert_std, tick, VARIANCE)

@@ -102,26 +102,22 @@ def tile_gnnnicheencoder_pa_t_kernel(
         sums = {}
         live = {}
 
-        def load_chunk(chunk):
-            first, first_new, end = chunk_tiles(chunk)
-            span = first // SPAN_TILES
-            if chunk % CHUNKS_PER_SPAN == 0:
+        def load_tiles(first, end):
+            span, T = divmod(first, SPAN_TILES)
+            if T == 0:
                 h_rows[span] = h_pool.tile([P, SPAN_TILES, D], BF16, name="h_rows")
             nc.sync.dma_start(
-                out=h_rows[span][:, first_new - SPAN_TILES * span : end - SPAN_TILES * span, :],
-                in_=h_flat[P * first_new : P * end, :].rearrange("(T p) f -> p T f", p=P),
+                out=h_rows[span][:, T : T + end - first, :],
+                in_=h_flat[P * first : P * end, :].rearrange("(T p) f -> p T f", p=P),
             )
 
-        for chunk in range(CHUNKS):
+        for x in range(chunk_tiles(0)[2]):
+            load_tiles(x, x + 1)
+        for chunk in range(1, CHUNKS):
             if chunk_tiles(chunk)[1] < LOAD_LEAD:
-                load_chunk(chunk)
+                load_tiles(chunk_tiles(chunk)[1], chunk_tiles(chunk)[2])
         wl_words, wl_plane = load_weight(nc, consts, W_l_words, W_l_scales, "wl")
         wr_words, wr_plane = load_weight(nc, consts, W_r_words, W_r_scales, "wr")
-        bias_rows = consts.tile([P, D], BF16, name="bias_rows")
-        nc.scalar.dma_start(out=bias_rows[:], in_=b_l.partition_broadcast(P))
-
-        ident = consts.tile([P, P], F32, name="ident")
-        make_identity(nc, ident[:])
 
         affine_rows = consts.tile([P, P], BF16, name="affine_rows")
         nc.vector.memset(affine_rows[:], 0.0)
@@ -129,16 +125,10 @@ def tile_gnnnicheencoder_pa_t_kernel(
         nc.scalar.dma_start(
             out=affine_rows[FEATURE_BLOCKS : 2 * FEATURE_BLOCKS, :], in_=ln_b.rearrange("(j p) -> j p", p=P)
         )
-        affine_rows_f32 = consts.tile([P, P], F32, name="affine_rows_f32")
-        nc.vector.tensor_copy(out=affine_rows_f32[:], in_=affine_rows[:])
-        affine_ps = turn_psum.tile([P, P], F32, name="affine_ps", tag="turned")
-        nc.tensor.transpose(affine_ps[:], affine_rows_f32[:], ident[:])
-        affine_cols = consts.tile([P, 2 * FEATURE_BLOCKS], F32, name="affine_cols")
-        nc.vector.tensor_copy(out=affine_cols[:], in_=affine_ps[:, 0 : 2 * FEATURE_BLOCKS])
-        relu_cols = consts.tile([P, 2 * FEATURE_BLOCKS], F32, name="relu_cols")
-        nc.vector.tensor_scalar_mul(out=relu_cols[:], in0=affine_cols[:], scalar1=1.0 - LEAKY_SLOPE)
-        line_cols = consts.tile([P, 2 * FEATURE_BLOCKS], F32, name="line_cols")
-        nc.vector.tensor_scalar_mul(out=line_cols[:], in0=affine_cols[:], scalar1=LEAKY_SLOPE)
+        bias_rows = consts.tile([P, D], BF16, name="bias_rows")
+        nc.scalar.dma_start(out=bias_rows[:], in_=b_l.partition_broadcast(P))
+        eps_col = consts.tile([P, 1], F32, name="eps_col")
+        nc.vector.memset(eps_col[:], LN_EPS)
 
         member_shape = [P, CHUNKS_PER_SPAN, CHUNK_TILES, CHUNK_GRAPHS]
         row_in_graph = consts.tile(member_shape, I32, name="row_in_graph")
@@ -164,8 +154,23 @@ def tile_gnnnicheencoder_pa_t_kernel(
             op0=ALU.is_le,
             op1=ALU.mult,
         )
-        eps_col = consts.tile([P, 1], F32, name="eps_col")
-        nc.vector.memset(eps_col[:], LN_EPS)
+        ident = consts.tile([P, P], F32, name="ident")
+        make_identity(nc, ident[:])
+
+        relu_cols = consts.tile([P, 2 * FEATURE_BLOCKS], F32, name="relu_cols")
+        line_cols = consts.tile([P, 2 * FEATURE_BLOCKS], F32, name="line_cols")
+
+        def prepare_affine_columns():
+            affine_rows_f32 = consts.tile([P, P], F32, name="affine_rows_f32")
+            nc.vector.tensor_copy(out=affine_rows_f32[:], in_=affine_rows[:])
+            affine_ps = back_psum.tile([P, P], F32, name="affine_ps", tag="a_rows")
+            nc.tensor.transpose(affine_ps[:], affine_rows_f32[:], ident[:])
+            nc.vector.tensor_scalar_mul(
+                out=relu_cols[:], in0=affine_ps[:, 0 : 2 * FEATURE_BLOCKS], scalar1=1.0 - LEAKY_SLOPE
+            )
+            nc.vector.tensor_scalar_mul(
+                out=line_cols[:], in0=affine_ps[:, 0 : 2 * FEATURE_BLOCKS], scalar1=LEAKY_SLOPE
+            )
 
         def turn_h(x):
             span, T = divmod(x, SPAN_TILES)
@@ -368,10 +373,10 @@ def tile_gnnnicheencoder_pa_t_kernel(
             if chunk is not None:
                 step(chunk)
 
-        for tick in range(ROW_TILES + RESIDUAL):
+        def run_tick(tick):
             chunk = chunk_by_first_new_tile.get(tick + LOAD_LEAD)
             if chunk is not None:
-                load_chunk(chunk)
+                load_tiles(chunk_tiles(chunk)[1], chunk_tiles(chunk)[2])
             for_tile(turn_h, tick, TURN_H)
             for_tile(turn_back, tick, TURN_BACK)
             for_tile(lambda x: sum_lane(x, 0, LANE_HEAD), tick, TURN_H)
@@ -390,3 +395,9 @@ def tile_gnnnicheencoder_pa_t_kernel(
             for_tile(sum_squares, tick, VARIANCE)
             for_tile(affine_and_split, tick, AFFINE)
             for_tile(invert_std, tick, VARIANCE)
+
+        for tick in range(MULTIPLY):
+            run_tick(tick)
+        prepare_affine_columns()
+        for tick in range(MULTIPLY, ROW_TILES + RESIDUAL):
+            run_tick(tick)

@@ -287,7 +287,7 @@ def tile_gnnnicheencoder_pa_t_kernel(
         def normalise(x):
             z = work.tile([P, D], F32, name="z")
             live["z", x] = z
-            nc.vector.tensor_scalar(
+            nc.gpsimd.tensor_scalar(
                 out=z[:],
                 in0=live["c", x][:],
                 scalar1=live["neg_mean", x][:],

@@ -27,6 +27,8 @@ CHUNK_ROWS = CHUNK_GRAPHS * NODES
 CHUNKS_PER_SPAN = SPAN_ROWS // CHUNK_ROWS
 CHUNKS = ROWS // CHUNK_ROWS
 CHUNK_TILES = 5
+PAIR = 2
+HALF_BLOCKS = FEATURE_BLOCKS // 2
 LANE_HEAD = 3
 LN_EPS = 1e-5
 LEAKY_SLOPE = 0.01
@@ -44,7 +46,7 @@ VARIANCE = ADD_BIAS + 1
 NORMALISE = VARIANCE + 1
 TURN_Z = NORMALISE + 1
 AFFINE = TURN_Z + 1
-TURN_BACK = AFFINE + 1
+TURN_BACK = AFFINE + 3
 RESIDUAL = TURN_BACK + 1
 
 FLOPS = 2 * 2 * ROWS * D * D
@@ -88,6 +90,8 @@ def tile_gnnnicheencoder_pa_t_kernel(
         span_pool = ctx.enter_context(tc.tile_pool(name="span_pool", bufs=2))
         c_pool = ctx.enter_context(tc.tile_pool(name="c_pool", bufs=5))
         work = ctx.enter_context(tc.tile_pool(name="work", bufs=3))
+        z_pool = ctx.enter_context(tc.tile_pool(name="z_pool", bufs=5))
+        term_pool = ctx.enter_context(tc.tile_pool(name="term_pool", bufs=2))
         stats = ctx.enter_context(tc.tile_pool(name="stats", bufs=6))
         turn_psum = ctx.enter_context(tc.psum_pool(name="turn_psum", bufs=2))
         acc_psum = ctx.enter_context(tc.psum_pool(name="acc_psum", bufs=2))
@@ -217,22 +221,37 @@ def tile_gnnnicheencoder_pa_t_kernel(
                 stop=True,
             )
 
-        def turn_z(x):
-            z_turned = zt_psum.tile([P, FEATURE_BLOCKS, P], F32, name="z_turned")
-            live["z_turned", x] = z_turned
-            for j in range(FEATURE_BLOCKS):
-                nc.tensor.transpose(z_turned[:, j, :], live["z", x][:, P * j : P * (j + 1)], ident[:])
+        def turn_z(pair, half):
+            z_turned = zt_psum.tile([P, HALF_BLOCKS, PAIR, P], F32, name="z_turned")
+            live["z_turned", pair, half] = z_turned
+            for jj in range(HALF_BLOCKS):
+                j = HALF_BLOCKS * half + jj
+                for i in range(PAIR):
+                    nc.tensor.transpose(
+                        z_turned[:, jj, i, :], live["z", PAIR * pair + i][:, P * j : P * (j + 1)], ident[:]
+                    )
 
         def turn_back(x):
             a_rows = back_psum.tile([P, D], F32, name="a_rows")
             live["a_rows", x] = a_rows
+            pair, i = divmod(x, PAIR)
             for j in range(FEATURE_BLOCKS):
                 block = a_rows[:, P * j : P * (j + 1)]
                 nc.tensor.matmul(
-                    out=block, lhsT=live["relu_term", x][:, j, :], rhs=ident[:], is_transpose=True, start=True, stop=False
+                    out=block,
+                    lhsT=live["relu_term", pair][:, j, i, :],
+                    rhs=ident[:],
+                    is_transpose=True,
+                    start=True,
+                    stop=False,
                 )
                 nc.tensor.matmul(
-                    out=block, lhsT=live["line_term", x][:, j, :], rhs=ident[:], is_transpose=True, start=False, stop=True
+                    out=block,
+                    lhsT=live["line_term", pair][:, j, i, :],
+                    rhs=ident[:],
+                    is_transpose=True,
+                    start=False,
+                    stop=True,
                 )
 
         def quantise(operand, grouped, x):
@@ -285,7 +304,7 @@ def tile_gnnnicheencoder_pa_t_kernel(
             )
 
         def normalise(x):
-            z = work.tile([P, D], F32, name="z")
+            z = z_pool.tile([P, D], F32, name="z")
             live["z", x] = z
             nc.gpsimd.tensor_scalar(
                 out=z[:],
@@ -346,16 +365,16 @@ def tile_gnnnicheencoder_pa_t_kernel(
                 out=rstd[:], in_=live["sq_sum", x][:], func=ACT.Abs_reciprocal_sqrt, bias=eps_col[:], scale=1.0 / D
             )
 
-        def affine_and_split(x):
-            relu_term = work.tile([P, FEATURE_BLOCKS, P], F32, name="relu_term")
-            line_term = work.tile([P, FEATURE_BLOCKS, P], F32, name="line_term")
-            live["relu_term", x] = relu_term
-            live["line_term", x] = line_term
-            for term, func, cols in ((relu_term, ACT.Relu, relu_cols), (line_term, ACT.Identity, line_cols)):
-                for j in range(FEATURE_BLOCKS):
+        def affine_and_split(pair, half):
+            if half == 0:
+                live["relu_term", pair] = term_pool.tile([P, FEATURE_BLOCKS, PAIR, P], F32, name="relu_term")
+                live["line_term", pair] = term_pool.tile([P, FEATURE_BLOCKS, PAIR, P], F32, name="line_term")
+            for kind, func, cols in (("relu_term", ACT.Relu, relu_cols), ("line_term", ACT.Identity, line_cols)):
+                for jj in range(HALF_BLOCKS):
+                    j = HALF_BLOCKS * half + jj
                     nc.scalar.activation(
-                        out=term[:, j, :],
-                        in_=live["z_turned", x][:, j, :],
+                        out=live[kind, pair][:, j, :, :].rearrange("p i r -> p (i r)"),
+                        in_=live["z_turned", pair, half][:, jj, :, :].rearrange("p i r -> p (i r)"),
                         func=func,
                         bias=cols[:, FEATURE_BLOCKS + j : FEATURE_BLOCKS + j + 1],
                         scale=cols[:, j : j + 1],
@@ -367,6 +386,11 @@ def tile_gnnnicheencoder_pa_t_kernel(
         def for_tile(step, tick, lag):
             if 0 <= tick - lag < ROW_TILES:
                 step(tick - lag)
+
+        def for_half_pair(step, tick, lag):
+            pair, half = divmod(tick - lag - (PAIR - 1), PAIR)
+            if 0 <= pair < ROW_TILES // PAIR:
+                step(pair, half)
 
         def for_chunk(step, tick, lag):
             chunk = chunk_by_last_tile.get(tick - lag)
@@ -382,7 +406,7 @@ def tile_gnnnicheencoder_pa_t_kernel(
             for_tile(lambda x: sum_lane(x, 0, LANE_HEAD), tick, TURN_H)
             for_tile(multiply, tick, MULTIPLY)
             for_tile(lambda x: sum_lane(x, LANE_HEAD, CHUNK_TILES), tick, TURN_H)
-            for_tile(turn_z, tick, TURN_Z)
+            for_half_pair(turn_z, tick, TURN_Z)
             for_tile(residual_and_store, tick, RESIDUAL)
             for_tile(add_bias, tick, ADD_BIAS)
             for_tile(normalise, tick, NORMALISE)
@@ -393,7 +417,7 @@ def tile_gnnnicheencoder_pa_t_kernel(
             for_tile(negate_mean, tick, VARIANCE)
             for_tile(copy_h, tick, COPY_H)
             for_tile(sum_squares, tick, VARIANCE)
-            for_tile(affine_and_split, tick, AFFINE)
+            for_half_pair(affine_and_split, tick, AFFINE)
             for_tile(invert_std, tick, VARIANCE)
 
         for tick in range(MULTIPLY):

@@ -27,6 +27,9 @@ CHUNK_ROWS = CHUNK_GRAPHS * NODES
 CHUNKS_PER_SPAN = SPAN_ROWS // CHUNK_ROWS
 CHUNKS = ROWS // CHUNK_ROWS
 CHUNK_TILES = 5
+PIECES = 4
+PIECE_GRAPHS = CHUNK_GRAPHS // PIECES
+PIECE_ROWS = PIECE_GRAPHS * NODES
 PAIR = 2
 HALF_BLOCKS = FEATURE_BLOCKS // 2
 LANE_HEAD = 3
@@ -266,27 +269,28 @@ def tile_gnnnicheencoder_pa_t_kernel(
                 in_=grouped[span][:, rows, :].rearrange("p r t -> p (r t)"),
             )
 
-        def chunk_of(grouped, chunk):
+        def piece_of(grouped, chunk, piece):
             span, q = divmod(chunk, CHUNKS_PER_SPAN)
-            return grouped[span][:, CHUNK_ROWS * q : CHUNK_ROWS * (q + 1), :]
+            first_row = CHUNK_ROWS * q + PIECE_ROWS * piece
+            return grouped[span][:, first_row : first_row + PIECE_ROWS, :]
 
-        def subtract(chunk):
+        def subtract(chunk, piece):
             span, q = divmod(chunk, CHUNKS_PER_SPAN)
-            if q == 0:
+            if q == 0 and piece == 0:
                 m_grouped[span] = span_pool.tile([P, SPAN_ROWS, PACK], BF16, name="m_grouped", align_bytes=64)
             nc.vector.tensor_tensor(
-                out=chunk_of(m_grouped, chunk).rearrange("p (g n) t -> p g n t", n=NODES),
-                in0=sums[chunk][:]
+                out=piece_of(m_grouped, chunk, piece).rearrange("p (g n) t -> p g n t", n=NODES),
+                in0=sums[chunk][:, :, PIECE_GRAPHS * piece : PIECE_GRAPHS * (piece + 1)]
                 .rearrange("p t g -> p g t")
                 .unsqueeze(2)
-                .to_broadcast([P, CHUNK_GRAPHS, NODES, PACK]),
-                in1=chunk_of(h_grouped, chunk).rearrange("p (g n) t -> p g n t", n=NODES),
+                .to_broadcast([P, PIECE_GRAPHS, NODES, PACK]),
+                in1=piece_of(h_grouped, chunk, piece).rearrange("p (g n) t -> p g n t", n=NODES),
                 op=ALU.subtract,
             )
 
-        def divide(chunk):
-            m_chunk = chunk_of(m_grouped, chunk).rearrange("p r t -> p (r t)")
-            nc.vector.tensor_scalar_mul(out=m_chunk, in0=m_chunk, scalar1=1.0 / (NODES - 1))
+        def divide(chunk, piece):
+            m_piece = piece_of(m_grouped, chunk, piece).rearrange("p r t -> p (r t)")
+            nc.vector.tensor_scalar_mul(out=m_piece, in0=m_piece, scalar1=1.0 / (NODES - 1))
 
         def add_bias(x):
             c = c_pool.tile([P, D], F32, name="c")
@@ -393,9 +397,10 @@ def tile_gnnnicheencoder_pa_t_kernel(
                 step(pair, half)
 
         def for_chunk(step, tick, lag):
-            chunk = chunk_by_last_tile.get(tick - lag)
-            if chunk is not None:
-                step(chunk)
+            for piece in range(PIECES):
+                chunk = chunk_by_last_tile.get(tick - lag - piece)
+                if chunk is not None:
+                    step(chunk, piece)
 
         def run_tick(tick):
             chunk = chunk_by_first_new_tile.get(tick + LOAD_LEAD)

@@ -369,19 +369,25 @@ def tile_gnnnicheencoder_pa_t_kernel(
                 out=rstd[:], in_=live["sq_sum", x][:], func=ACT.Abs_reciprocal_sqrt, bias=eps_col[:], scale=1.0 / D
             )
 
-        def affine_and_split(pair, half):
+        def affine_term(pair, half, kind, on_vector):
             if half == 0:
-                live["relu_term", pair] = term_pool.tile([P, FEATURE_BLOCKS, PAIR, P], F32, name="relu_term")
-                live["line_term", pair] = term_pool.tile([P, FEATURE_BLOCKS, PAIR, P], F32, name="line_term")
-            for kind, func, cols in (("relu_term", ACT.Relu, relu_cols), ("line_term", ACT.Identity, line_cols)):
-                for jj in range(HALF_BLOCKS):
-                    j = HALF_BLOCKS * half + jj
+                live[kind, pair] = term_pool.tile([P, FEATURE_BLOCKS, PAIR, P], F32, name=kind)
+            cols = relu_cols if kind == "relu_term" else line_cols
+            for jj in range(HALF_BLOCKS):
+                j = HALF_BLOCKS * half + jj
+                term = live[kind, pair][:, j, :, :].rearrange("p i r -> p (i r)")
+                z_block = live["z_turned", pair, half][:, jj, :, :].rearrange("p i r -> p (i r)")
+                gain = cols[:, j : j + 1]
+                shift = cols[:, FEATURE_BLOCKS + j : FEATURE_BLOCKS + j + 1]
+                if on_vector:
+                    nc.vector.tensor_scalar(out=term, in0=z_block, scalar1=gain, scalar2=shift, op0=ALU.mult, op1=ALU.add)
+                else:
                     nc.scalar.activation(
-                        out=live[kind, pair][:, j, :, :].rearrange("p i r -> p (i r)"),
-                        in_=live["z_turned", pair, half][:, jj, :, :].rearrange("p i r -> p (i r)"),
-                        func=func,
-                        bias=cols[:, FEATURE_BLOCKS + j : FEATURE_BLOCKS + j + 1],
-                        scale=cols[:, j : j + 1],
+                        out=term,
+                        in_=z_block,
+                        func=ACT.Relu if kind == "relu_term" else ACT.Identity,
+                        bias=shift,
+                        scale=gain,
                     )
 
         chunk_by_first_new_tile = {chunk_tiles(chunk)[1]: chunk for chunk in range(CHUNKS)}
@@ -419,10 +425,15 @@ def tile_gnnnicheencoder_pa_t_kernel(
             for_tile(lambda x: quantise("m", m_grouped, x), tick, QUANTISE_M)
             for_chunk(divide, tick, DIVIDE)
             for_chunk(subtract, tick, SUBTRACT)
+            line_on_vector = tick >= ROW_TILES - 1 + QUANTISE_M
+            if line_on_vector:
+                for_half_pair(lambda pair, half: affine_term(pair, half, "line_term", True), tick, AFFINE)
             for_tile(negate_mean, tick, VARIANCE)
             for_tile(copy_h, tick, COPY_H)
             for_tile(sum_squares, tick, VARIANCE)
-            for_half_pair(affine_and_split, tick, AFFINE)
+            for_half_pair(lambda pair, half: affine_term(pair, half, "relu_term", False), tick, AFFINE)
+            if not line_on_vector:
+                for_half_pair(lambda pair, half: affine_term(pair, half, "line_term", False), tick, AFFINE)
             for_tile(invert_std, tick, VARIANCE)
 
         for tick in range(MULTIPLY):

@@ -20,30 +20,26 @@ D = 512
 FEATURE_BLOCKS = D // P
 ROWS = GRAPHS * NODES
 ROW_TILES = ROWS // P
+CELL_GRAPHS = 32
+FOLD = P // CELL_GRAPHS
+CELL_TILES = 4
+CELLS = GRAPHS // CELL_GRAPHS
+SPAN_CELLS = P // CELL_GRAPHS
 SPAN_TILES = NODES
-SPAN_ROWS = SPAN_TILES * P
-CHUNK_GRAPHS = 32
-CHUNK_ROWS = CHUNK_GRAPHS * NODES
-CHUNKS_PER_SPAN = SPAN_ROWS // CHUNK_ROWS
-CHUNKS = ROWS // CHUNK_ROWS
-CHUNK_TILES = 5
-PIECES = 4
-PIECE_GRAPHS = CHUNK_GRAPHS // PIECES
-PIECE_ROWS = PIECE_GRAPHS * NODES
+LAST = SPAN_TILES - 1
+SPANS = ROW_TILES // SPAN_TILES
 PAIR = 2
 HALF_BLOCKS = FEATURE_BLOCKS // 2
 LANE_HEAD = 3
 LN_EPS = 1e-5
 LEAKY_SLOPE = 0.01
 
-LOAD_LEAD = 8
-TURN_H = 0
+LOAD = -10
+TURN_H = -2
 COPY_H = TURN_H + 1
-QUANTISE_H = COPY_H + 1
-SUBTRACT = COPY_H + 1
-DIVIDE = SUBTRACT + 1
-QUANTISE_M = (CHUNK_TILES - 1) + DIVIDE + 1
-MULTIPLY = QUANTISE_M + 1
+MEAN = COPY_H + 1
+QUANTISE = MEAN + 1
+MULTIPLY = QUANTISE + 1
 ADD_BIAS = MULTIPLY + 1
 VARIANCE = ADD_BIAS + 1
 NORMALISE = VARIANCE + 1
@@ -51,15 +47,9 @@ TURN_Z = NORMALISE + 1
 AFFINE = TURN_Z + 1
 TURN_BACK = AFFINE + 3
 RESIDUAL = TURN_BACK + 1
+SUMS = MEAN - CELL_TILES
 
 FLOPS = 2 * 2 * ROWS * D * D
-
-
-def chunk_tiles(chunk):
-    span, q = divmod(chunk, CHUNKS_PER_SPAN)
-    first_row = CHUNK_ROWS * q
-    base = SPAN_TILES * span
-    return base + first_row // P, base - (-first_row // P), base - (-(first_row + CHUNK_ROWS) // P)
 
 
 def load_weight(nc, pool, words_dram, scales_dram, label):
@@ -79,52 +69,98 @@ def load_weight(nc, pool, words_dram, scales_dram, label):
     return words, plane
 
 
+def cell_of(x):
+    span, T = divmod(x, SPAN_TILES)
+    return SPAN_CELLS * span + T // CELL_TILES, T % CELL_TILES
+
+
+def is_last(x):
+    return x % SPAN_TILES == LAST
+
+
 def tile_gnnnicheencoder_pa_t_kernel(
     tc, h, W_l_words, W_l_scales, b_l, W_r_words, W_r_scales, ln_g, ln_b, out
 ):
     nc = tc.nc
-    h_flat = h.flatten_outer_dims()
-    out_flat = out.flatten_outer_dims()
 
     with ExitStack() as ctx:
         ctx.enter_context(tc.manual_schedule())
         consts = ctx.enter_context(tc.tile_pool(name="consts", bufs=1))
-        h_pool = ctx.enter_context(tc.tile_pool(name="h_pool", bufs=3))
-        span_pool = ctx.enter_context(tc.tile_pool(name="span_pool", bufs=2))
+        cell_pool = ctx.enter_context(tc.tile_pool(name="cell_pool", bufs=8))
+        last_pool = ctx.enter_context(tc.tile_pool(name="last_pool", bufs=4))
+        pair_pool = ctx.enter_context(tc.tile_pool(name="pair_pool", bufs=6))
+        last_pair_pool = ctx.enter_context(tc.tile_pool(name="last_pair_pool", bufs=2))
+        code_pool = ctx.enter_context(tc.tile_pool(name="code_pool", bufs=4))
         c_pool = ctx.enter_context(tc.tile_pool(name="c_pool", bufs=5))
-        work = ctx.enter_context(tc.tile_pool(name="work", bufs=3))
-        z_pool = ctx.enter_context(tc.tile_pool(name="z_pool", bufs=5))
-        term_pool = ctx.enter_context(tc.tile_pool(name="term_pool", bufs=2))
+        work = ctx.enter_context(tc.tile_pool(name="work", bufs=4))
+        z_pool = ctx.enter_context(tc.tile_pool(name="z_pool", bufs=6))
+        term_pool = ctx.enter_context(tc.tile_pool(name="term_pool", bufs=3))
         stats = ctx.enter_context(tc.tile_pool(name="stats", bufs=6))
-        turn_psum = ctx.enter_context(tc.psum_pool(name="turn_psum", bufs=2))
-        acc_psum = ctx.enter_context(tc.psum_pool(name="acc_psum", bufs=2))
+        turn_psum = ctx.enter_context(tc.psum_pool(name="turn_psum", bufs=1))
+        acc_psum = ctx.enter_context(tc.psum_pool(name="acc_psum", bufs=1))
+        sums_psum = ctx.enter_context(tc.psum_pool(name="sums_psum", bufs=2))
         zt_psum = ctx.enter_context(tc.psum_pool(name="zt_psum", bufs=2))
         back_psum = ctx.enter_context(tc.psum_pool(name="back_psum", bufs=2))
 
-        h_rows = {}
-        h_grouped = {}
-        m_grouped = {}
-        words = {}
-        planes = {}
-        sums = {}
+        cell_rows = {}
+        last_rows = {}
         live = {}
 
-        def load_tiles(first, end):
-            span, T = divmod(first, SPAN_TILES)
-            if T == 0:
-                h_rows[span] = h_pool.tile([P, SPAN_TILES, D], BF16, name="h_rows")
-            nc.sync.dma_start(
-                out=h_rows[span][:, T : T + end - first, :],
-                in_=h_flat[P * first : P * end, :].rearrange("(T p) f -> p T f", p=P),
-            )
+        def rows_of(x):
+            if is_last(x):
+                return last_rows[x // SPAN_TILES][:]
+            cell, j = cell_of(x)
+            return cell_rows[cell][:, j, :]
 
-        for x in range(chunk_tiles(0)[2]):
-            load_tiles(x, x + 1)
-        for chunk in range(1, CHUNKS):
-            if chunk_tiles(chunk)[1] < LOAD_LEAD:
-                load_tiles(chunk_tiles(chunk)[1], chunk_tiles(chunk)[2])
+        def load_last(span):
+            last_rows[span] = last_pool.tile([P, D], BF16, name="last_rows")
+            nc.sync.dma_start(out=last_rows[span][:], in_=h[P * span : P * (span + 1), NODES - 1, :])
+
+        def load_cell(cell):
+            cell_rows[cell] = cell_pool.tile([P, CELL_TILES, D], BF16, name="cell_rows")
+            graphs = slice(CELL_GRAPHS * cell, CELL_GRAPHS * (cell + 1))
+            for a in range(FOLD):
+                nc.sync.dma_start(
+                    out=cell_rows[cell][CELL_GRAPHS * a : CELL_GRAPHS * (a + 1), :, :],
+                    in_=h[graphs, CELL_TILES * a : CELL_TILES * (a + 1), :],
+                )
+
+        load_last(0)
+        load_cell(0)
+        load_cell(1)
         wl_words, wl_plane = load_weight(nc, consts, W_l_words, W_l_scales, "wl")
         wr_words, wr_plane = load_weight(nc, consts, W_r_words, W_r_scales, "wr")
+        load_cell(2)
+
+        ident = consts.tile([P, P], F32, name="ident")
+        make_identity(nc, ident[:])
+
+        offset = consts.tile([P, SPAN_CELLS, CELL_GRAPHS], I32, name="offset")
+        nc.gpsimd.iota(
+            offset[:], pattern=[[-CELL_GRAPHS, SPAN_CELLS], [-1, CELL_GRAPHS]], base=0, channel_multiplier=1
+        )
+        pick = consts.tile([P, SPAN_CELLS, CELL_GRAPHS], BF16, name="pick")
+        nc.vector.tensor_scalar(
+            out=pick[:].rearrange("p q g -> p (q g)"),
+            in0=offset[:].rearrange("p q g -> p (q g)"),
+            scalar1=0.0,
+            scalar2=1.0 / (NODES - 1),
+            op0=ALU.is_equal,
+            op1=ALU.mult,
+        )
+        fold = consts.tile([P, CELL_GRAPHS], BF16, name="fold")
+        offset_in_cell = consts.tile([P, CELL_GRAPHS], I32, name="offset_in_cell")
+        nc.vector.tensor_single_scalar(
+            out=offset_in_cell[:], in_=offset[:, 0, :], scalar=CELL_GRAPHS - 1, op=ALU.bitwise_and
+        )
+        nc.vector.tensor_scalar(
+            out=fold[:],
+            in0=offset_in_cell[:],
+            scalar1=0.0,
+            scalar2=1.0 / (NODES - 1),
+            op0=ALU.is_equal,
+            op1=ALU.mult,
+        )
 
         affine_rows = consts.tile([P, P], BF16, name="affine_rows")
         nc.vector.memset(affine_rows[:], 0.0)
@@ -136,33 +172,6 @@ def tile_gnnnicheencoder_pa_t_kernel(
         nc.scalar.dma_start(out=bias_rows[:], in_=b_l.partition_broadcast(P))
         eps_col = consts.tile([P, 1], F32, name="eps_col")
         nc.vector.memset(eps_col[:], LN_EPS)
-
-        member_shape = [P, CHUNKS_PER_SPAN, CHUNK_TILES, CHUNK_GRAPHS]
-        row_in_graph = consts.tile(member_shape, I32, name="row_in_graph")
-        nc.gpsimd.iota(
-            row_in_graph[:],
-            pattern=[[(CHUNK_ROWS // P) * P - CHUNK_ROWS, CHUNKS_PER_SPAN], [P, CHUNK_TILES], [-NODES, CHUNK_GRAPHS]],
-            base=0,
-            channel_multiplier=1,
-        )
-        not_before = consts.tile(member_shape, BF16, name="not_before")
-        nc.vector.tensor_single_scalar(
-            out=not_before[:].rearrange("p q i g -> p (q i g)"),
-            in_=row_in_graph[:].rearrange("p q i g -> p (q i g)"),
-            scalar=0.0,
-            op=ALU.is_ge,
-        )
-        member = consts.tile(member_shape, BF16, name="member")
-        nc.vector.scalar_tensor_tensor(
-            out=member[:].rearrange("p q i g -> p (q i g)"),
-            in0=row_in_graph[:].rearrange("p q i g -> p (q i g)"),
-            scalar=float(NODES - 1),
-            in1=not_before[:].rearrange("p q i g -> p (q i g)"),
-            op0=ALU.is_le,
-            op1=ALU.mult,
-        )
-        ident = consts.tile([P, P], F32, name="ident")
-        make_identity(nc, ident[:])
 
         relu_cols = consts.tile([P, 2 * FEATURE_BLOCKS], F32, name="relu_cols")
         line_cols = consts.tile([P, 2 * FEATURE_BLOCKS], F32, name="line_cols")
@@ -180,49 +189,41 @@ def tile_gnnnicheencoder_pa_t_kernel(
             )
 
         def turn_h(x):
-            span, T = divmod(x, SPAN_TILES)
-            turned = turn_psum.tile([P, 2 * P + CHUNK_GRAPHS], F32, name="turned")
+            turned = turn_psum.tile([P, 2 * P], F32, name="turned")
             live["turned", x] = turned
-            pairs = h_rows[span][:, T, :].bitcast(F32)
+            pairs = rows_of(x).bitcast(F32)
             for u in range(2):
                 nc.tensor.transpose(turned[:, P * u : P * (u + 1)], pairs[:, u : D // 2 : 2], ident[:])
 
-        def sum_lane(x, first_part, end_part):
-            span, T = divmod(x, SPAN_TILES)
-            if T > 0:
-                q, t = divmod(T - 1, PACK)
-                for i in range(first_part, end_part):
-                    nc.tensor.matmul(
-                        out=live["turned", x][:, 2 * P :],
-                        lhsT=h_rows[span][:, (CHUNK_ROWS // P) * q + i, t:D:PACK],
-                        rhs=member[:, q, i, :],
-                        start=(i == 0),
-                        stop=(i == CHUNK_TILES - 1),
-                    )
+        def sum_lane(cell, t, first_part, end_part):
+            if t == 0 and first_part == 0:
+                live["sums", cell] = sums_psum.tile([P, CELL_GRAPHS, PACK], F32, name="sums")
+            span, q = divmod(cell, SPAN_CELLS)
+            for i in range(first_part, end_part):
+                rows = cell_rows[cell][:, i, :] if i < CELL_TILES else last_rows[span][:]
+                nc.tensor.matmul(
+                    out=live["sums", cell][:, :, t],
+                    lhsT=rows[:, t:D:PACK],
+                    rhs=fold[:] if i < CELL_TILES else pick[:, q, :],
+                    start=(i == 0),
+                    stop=(i == CELL_TILES),
+                )
 
         def multiply(x):
-            span, T = divmod(x, SPAN_TILES)
-            rows = slice(P * T, P * (T + 1))
             acc = acc_psum.tile([P, D], F32, name="acc")
             live["acc", x] = acc
-            nc.tensor.matmul_mx(
-                out=acc[:],
-                lhsT=words["m", span][:, rows].bitcast(FP8X4),
-                lhsT_scale=planes["m", span][:, rows],
-                rhs=wl_words[:].bitcast(FP8X4),
-                rhs_scale=wl_plane[:],
-                start=True,
-                stop=False,
-            )
-            nc.tensor.matmul_mx(
-                out=acc[:],
-                lhsT=words["h", span][:, rows].bitcast(FP8X4),
-                lhsT_scale=planes["h", span][:, rows],
-                rhs=wr_words[:].bitcast(FP8X4),
-                rhs_scale=wr_plane[:],
-                start=False,
-                stop=True,
-            )
+            words, plane = live["codes", x]
+            for operand, w_words, w_plane in ((1, wl_words, wl_plane), (0, wr_words, wr_plane)):
+                cols = slice(P * operand, P * (operand + 1))
+                nc.tensor.matmul_mx(
+                    out=acc[:],
+                    lhsT=words[:, cols].bitcast(FP8X4),
+                    lhsT_scale=plane[:, cols],
+                    rhs=w_words[:].bitcast(FP8X4),
+                    rhs_scale=w_plane[:],
+                    start=(operand == 1),
+                    stop=(operand == 0),
+                )
 
         def turn_z(pair, half):
             z_turned = zt_psum.tile([P, HALF_BLOCKS, PAIR, P], F32, name="z_turned")
@@ -257,40 +258,36 @@ def tile_gnnnicheencoder_pa_t_kernel(
                     stop=True,
                 )
 
-        def quantise(operand, grouped, x):
-            span, T = divmod(x, SPAN_TILES)
-            if T == 0:
-                words[operand, span] = span_pool.tile([P, SPAN_ROWS], U32, name=operand + "_words", align_bytes=64)
-                planes[operand, span] = span_pool.tile([P, SPAN_ROWS], U8, name=operand + "_plane", align_bytes=64)
-            rows = slice(P * T, P * (T + 1))
+        def average_part(pair_tile, rows, cell, times):
+            shape = [P, times, CELL_GRAPHS * PACK]
+            nc.vector.scalar_tensor_tensor(
+                out=pair_tile[:, 1, rows, :].rearrange("p (a g) t -> p a (g t)", a=times),
+                in0=pair_tile[:, 0, rows, :].rearrange("p (a g) t -> p a (g t)", a=times),
+                scalar=-1.0 / (NODES - 1),
+                in1=live["sums", cell][:].rearrange("p g t -> p (g t)").unsqueeze(1).to_broadcast(shape),
+                op0=ALU.mult,
+                op1=ALU.add,
+            )
+
+        def average(x):
+            if is_last(x):
+                return
+            cell, j = cell_of(x)
+            average_part(live["hm", x], slice(0, P), cell, FOLD)
+            if j == CELL_TILES - 1:
+                span, q = divmod(cell, SPAN_CELLS)
+                rows = slice(CELL_GRAPHS * q, CELL_GRAPHS * (q + 1))
+                average_part(live["hm", SPAN_TILES * span + LAST], rows, cell, 1)
+
+        def quantise(x):
+            words = code_pool.tile([P, 2 * P], U32, name="words", align_bytes=64)
+            plane = code_pool.tile([P, 2 * P], U8, name="plane", align_bytes=64)
+            live["codes", x] = words, plane
             nc.vector.quantize_mx(
-                out=words[operand, span][:, rows].bitcast(FP8X4),
-                scales=planes[operand, span][:, rows],
-                in_=grouped[span][:, rows, :].rearrange("p r t -> p (r t)"),
+                out=words[:].bitcast(FP8X4),
+                scales=plane[:],
+                in_=live["hm", x][:].rearrange("p o r t -> p (o r t)"),
             )
-
-        def piece_of(grouped, chunk, piece):
-            span, q = divmod(chunk, CHUNKS_PER_SPAN)
-            first_row = CHUNK_ROWS * q + PIECE_ROWS * piece
-            return grouped[span][:, first_row : first_row + PIECE_ROWS, :]
-
-        def subtract(chunk, piece):
-            span, q = divmod(chunk, CHUNKS_PER_SPAN)
-            if q == 0 and piece == 0:
-                m_grouped[span] = span_pool.tile([P, SPAN_ROWS, PACK], BF16, name="m_grouped", align_bytes=64)
-            nc.vector.tensor_tensor(
-                out=piece_of(m_grouped, chunk, piece).rearrange("p (g n) t -> p g n t", n=NODES),
-                in0=sums[chunk][:, :, PIECE_GRAPHS * piece : PIECE_GRAPHS * (piece + 1)]
-                .rearrange("p t g -> p g t")
-                .unsqueeze(2)
-                .to_broadcast([P, PIECE_GRAPHS, NODES, PACK]),
-                in1=piece_of(h_grouped, chunk, piece).rearrange("p (g n) t -> p g n t", n=NODES),
-                op=ALU.subtract,
-            )
-
-        def divide(chunk, piece):
-            m_piece = piece_of(m_grouped, chunk, piece).rearrange("p r t -> p (r t)")
-            nc.vector.tensor_scalar_mul(out=m_piece, in0=m_piece, scalar1=1.0 / (NODES - 1))
 
         def add_bias(x):
             c = c_pool.tile([P, D], F32, name="c")
@@ -307,6 +304,28 @@ def tile_gnnnicheencoder_pa_t_kernel(
                 accum_out=row_sum[:],
             )
 
+        def residual_and_store(x):
+            result = work.tile([P, D], F32, name="result")
+            nc.vector.tensor_tensor(out=result[:], in0=live["a_rows", x][:], in1=rows_of(x), op=ALU.add)
+            if is_last(x):
+                span = x // SPAN_TILES
+                nc.sync.dma_start(out=out[P * span : P * (span + 1), NODES - 1, :], in_=result[:])
+            else:
+                cell, j = cell_of(x)
+                graphs = slice(CELL_GRAPHS * cell, CELL_GRAPHS * (cell + 1))
+                for a in range(FOLD):
+                    nc.sync.dma_start(
+                        out=out[graphs, CELL_TILES * a + j, :],
+                        in_=result[CELL_GRAPHS * a : CELL_GRAPHS * (a + 1), :],
+                    )
+
+        def negate_mean(x):
+            neg_mean = stats.tile([P, 1], F32, name="neg_mean")
+            live["neg_mean", x] = neg_mean
+            nc.gpsimd.tensor_scalar(
+                out=neg_mean[:], in0=live["row_sum", x][:], scalar1=-1.0 / D, scalar2=0.0, op0=ALU.mult, op1=ALU.add
+            )
+
         def normalise(x):
             z = z_pool.tile([P, D], F32, name="z")
             live["z", x] = z
@@ -319,35 +338,14 @@ def tile_gnnnicheencoder_pa_t_kernel(
                 op1=ALU.mult,
             )
 
-        def residual_and_store(x):
-            span, T = divmod(x, SPAN_TILES)
-            result = work.tile([P, D], F32, name="result")
-            nc.vector.tensor_tensor(out=result[:], in0=live["a_rows", x][:], in1=h_rows[span][:, T, :], op=ALU.add)
-            nc.sync.dma_start(out=out_flat[P * x : P * (x + 1), :], in_=result[:])
-
         def copy_h(x):
-            span, T = divmod(x, SPAN_TILES)
-            if T == 0:
-                h_grouped[span] = span_pool.tile([P, SPAN_ROWS, PACK], BF16, name="h_grouped", align_bytes=64)
-            turned = live["turned", x]
+            pool = last_pair_pool if is_last(x) else pair_pool
+            hm = pool.tile([P, 2, P, PACK], BF16, name="hm", align_bytes=64)
+            live["hm", x] = hm
             nc.scalar.copy(
-                out=h_grouped[span][:, P * T : P * (T + 1), :]
-                .rearrange("p r t -> p (r t)")
-                .bitcast(F32)
-                .rearrange("p (r u) -> p r u", u=2),
-                in_=turned[:, 0 : 2 * P].rearrange("p (u r) -> p r u", u=2),
+                out=hm[:, 0, :, :].rearrange("p r t -> p (r t)").bitcast(F32).rearrange("p (r u) -> p r u", u=2),
+                in_=live["turned", x][:].rearrange("p (u r) -> p r u", u=2),
             )
-            if T > 0:
-                q, t = divmod(T - 1, PACK)
-                chunk = CHUNKS_PER_SPAN * span + q
-                if t == 0:
-                    sums[chunk] = work.tile([P, PACK, CHUNK_GRAPHS], F32, name="sums")
-                nc.scalar.copy(out=sums[chunk][:, t, :], in_=turned[:, 2 * P :])
-
-        def negate_mean(x):
-            neg_mean = stats.tile([P, 1], F32, name="neg_mean")
-            live["neg_mean", x] = neg_mean
-            nc.scalar.mul(out=neg_mean[:], in_=live["row_sum", x][:], mul=-1.0 / D)
 
         def sum_squares(x):
             squares = work.tile([P, D], F32, name="squares")
@@ -357,8 +355,8 @@ def tile_gnnnicheencoder_pa_t_kernel(
                 out=squares[:],
                 in_=live["c", x][:],
                 func=ACT.Square,
-                bias=live["neg_mean", x][:],
-                scale=1.0,
+                bias=live["row_sum", x][:],
+                scale=-float(D),
                 accum_out=sq_sum[:],
             )
 
@@ -366,7 +364,11 @@ def tile_gnnnicheencoder_pa_t_kernel(
             rstd = stats.tile([P, 1], F32, name="rstd")
             live["rstd", x] = rstd
             nc.scalar.activation(
-                out=rstd[:], in_=live["sq_sum", x][:], func=ACT.Abs_reciprocal_sqrt, bias=eps_col[:], scale=1.0 / D
+                out=rstd[:],
+                in_=live["sq_sum", x][:],
+                func=ACT.Abs_reciprocal_sqrt,
+                bias=eps_col[:],
+                scale=1.0 / (D * D * D),
             )
 
         def affine_term(pair, half, kind, on_vector):
@@ -390,53 +392,62 @@ def tile_gnnnicheencoder_pa_t_kernel(
                         scale=gain,
                     )
 
-        chunk_by_first_new_tile = {chunk_tiles(chunk)[1]: chunk for chunk in range(CHUNKS)}
-        chunk_by_last_tile = {chunk_tiles(chunk)[2] - 1: chunk for chunk in range(CHUNKS)}
+        turning_order = {}
+        for x in range(ROW_TILES):
+            turning_order[x if not is_last(x) else x - SPAN_TILES] = x
+        first_tile = {SPAN_TILES * (cell // SPAN_CELLS) + CELL_TILES * (cell % SPAN_CELLS): cell for cell in range(CELLS)}
 
         def for_tile(step, tick, lag):
             if 0 <= tick - lag < ROW_TILES:
                 step(tick - lag)
+
+        def for_turning(step, tick, lag):
+            if tick - lag in turning_order:
+                step(turning_order[tick - lag])
 
         def for_half_pair(step, tick, lag):
             pair, half = divmod(tick - lag - (PAIR - 1), PAIR)
             if 0 <= pair < ROW_TILES // PAIR:
                 step(pair, half)
 
-        def for_chunk(step, tick, lag):
-            for piece in range(PIECES):
-                chunk = chunk_by_last_tile.get(tick - lag - piece)
-                if chunk is not None:
-                    step(chunk, piece)
+        def for_lane(tick, first_part, end_part):
+            for t in range(PACK):
+                cell = first_tile.get(tick - SUMS - t)
+                if cell is not None:
+                    sum_lane(cell, t, first_part, end_part)
+
+        def load(tick):
+            cell = first_tile.get(tick - LOAD)
+            if cell is not None and cell > 2:
+                if cell % SPAN_CELLS == 0:
+                    load_last(cell // SPAN_CELLS)
+                load_cell(cell)
 
         def run_tick(tick):
-            chunk = chunk_by_first_new_tile.get(tick + LOAD_LEAD)
-            if chunk is not None:
-                load_tiles(chunk_tiles(chunk)[1], chunk_tiles(chunk)[2])
-            for_tile(turn_h, tick, TURN_H)
-            for_tile(turn_back, tick, TURN_BACK)
-            for_tile(lambda x: sum_lane(x, 0, LANE_HEAD), tick, TURN_H)
-            for_tile(multiply, tick, MULTIPLY)
-            for_tile(lambda x: sum_lane(x, LANE_HEAD, CHUNK_TILES), tick, TURN_H)
-            for_half_pair(turn_z, tick, TURN_Z)
-            for_tile(residual_and_store, tick, RESIDUAL)
+            load(tick)
+            for_turning(copy_h, tick, COPY_H)
+            for_tile(sum_squares, tick, VARIANCE)
             for_tile(add_bias, tick, ADD_BIAS)
+            for_half_pair(turn_z, tick, TURN_Z)
+            for_tile(turn_back, tick, TURN_BACK)
+            for_turning(turn_h, tick, TURN_H)
+            for_lane(tick, 0, LANE_HEAD)
+            for_tile(multiply, tick, MULTIPLY)
+            for_lane(tick, LANE_HEAD, CELL_TILES + 1)
             for_tile(normalise, tick, NORMALISE)
-            for_tile(lambda x: quantise("h", h_grouped, x), tick, QUANTISE_H)
-            for_tile(lambda x: quantise("m", m_grouped, x), tick, QUANTISE_M)
-            for_chunk(divide, tick, DIVIDE)
-            for_chunk(subtract, tick, SUBTRACT)
-            line_on_vector = tick >= ROW_TILES - 1 + QUANTISE_M
+            for_tile(negate_mean, tick, VARIANCE)
+            for_tile(quantise, tick, QUANTISE)
+            for_tile(residual_and_store, tick, RESIDUAL)
+            for_tile(average, tick, MEAN)
+            line_on_vector = tick > ROW_TILES - 1 + QUANTISE
             if line_on_vector:
                 for_half_pair(lambda pair, half: affine_term(pair, half, "line_term", True), tick, AFFINE)
-            for_tile(negate_mean, tick, VARIANCE)
-            for_tile(copy_h, tick, COPY_H)
-            for_tile(sum_squares, tick, VARIANCE)
             for_half_pair(lambda pair, half: affine_term(pair, half, "relu_term", False), tick, AFFINE)
             if not line_on_vector:
                 for_half_pair(lambda pair, half: affine_term(pair, half, "line_term", False), tick, AFFINE)
             for_tile(invert_std, tick, VARIANCE)
 
-        for tick in range(MULTIPLY):
+        for tick in range(SUMS, MULTIPLY):
             run_tick(tick)
         prepare_affine_columns()
         for tick in range(MULTIPLY, ROW_TILES + RESIDUAL):

@@ -125,6 +125,19 @@ def tile_gnnnicheencoder_pa_t_kernel(
                     in_=h[graphs, CELL_TILES * a : CELL_TILES * (a + 1), :],
                 )
 
+        eps_col = consts.tile([P, 1], F32, name="eps_col")
+        nc.vector.memset(eps_col[:], LN_EPS)
+        table_col = consts.tile([P, 1], F32, name="table_col")
+        nc.scalar.activation(out=table_col[:], in_=eps_col[:], func=ACT.Abs_reciprocal_sqrt, bias=eps_col[:], scale=1.0)
+        bias_row = consts.tile([P, D], BF16, name="bias_row")
+        nc.vector.memset(bias_row[:], 0.0)
+        nc.scalar.dma_start(out=bias_row[0:1, :], in_=b_l.rearrange("(o f) -> o f", o=1))
+        affine_rows = consts.tile([P, P], BF16, name="affine_rows")
+        nc.vector.memset(affine_rows[:], 0.0)
+        nc.scalar.dma_start(out=affine_rows[0:FEATURE_BLOCKS, :], in_=ln_g.rearrange("(j p) -> j p", p=P))
+        nc.scalar.dma_start(
+            out=affine_rows[FEATURE_BLOCKS : 2 * FEATURE_BLOCKS, :], in_=ln_b.rearrange("(j p) -> j p", p=P)
+        )
         load_last(0)
         load_cell(0)
         load_cell(1)
@@ -162,34 +175,35 @@ def tile_gnnnicheencoder_pa_t_kernel(
             op1=ALU.mult,
         )
 
-        affine_rows = consts.tile([P, P], BF16, name="affine_rows")
-        nc.vector.memset(affine_rows[:], 0.0)
-        nc.scalar.dma_start(out=affine_rows[0:FEATURE_BLOCKS, :], in_=ln_g.rearrange("(j p) -> j p", p=P))
-        nc.scalar.dma_start(
-            out=affine_rows[FEATURE_BLOCKS : 2 * FEATURE_BLOCKS, :], in_=ln_b.rearrange("(j p) -> j p", p=P)
-        )
+        ones = consts.tile([P, P], BF16, name="ones")
+        nc.vector.memset(ones[:], 1.0)
         bias_rows = consts.tile([P, D], BF16, name="bias_rows")
-        nc.scalar.dma_start(out=bias_rows[:], in_=b_l.partition_broadcast(P))
-        eps_col = consts.tile([P, 1], F32, name="eps_col")
-        nc.vector.memset(eps_col[:], LN_EPS)
 
         relu_cols = consts.tile([P, 2 * FEATURE_BLOCKS], F32, name="relu_cols")
         line_cols = consts.tile([P, 2 * FEATURE_BLOCKS], F32, name="line_cols")
 
-        def prepare_affine_columns():
-            affine_rows_f32 = consts.tile([P, P], F32, name="affine_rows_f32")
-            nc.vector.tensor_copy(out=affine_rows_f32[:], in_=affine_rows[:])
-            affine_ps = back_psum.tile([P, P], F32, name="affine_ps", tag="a_rows")
-            nc.tensor.transpose(affine_ps[:], affine_rows_f32[:], ident[:])
-            nc.vector.tensor_scalar_mul(
-                out=relu_cols[:], in0=affine_ps[:, 0 : 2 * FEATURE_BLOCKS], scalar1=1.0 - LEAKY_SLOPE
-            )
-            nc.vector.tensor_scalar_mul(
-                out=line_cols[:], in0=affine_ps[:, 0 : 2 * FEATURE_BLOCKS], scalar1=LEAKY_SLOPE
-            )
+        affine_rows_f32 = consts.tile([P, P], F32, name="affine_rows_f32")
+
+        def prepare(tick):
+            if tick == MEAN:
+                live["bias"] = zt_psum.tile([P, D], F32, name="bias_ps", tag="z_turned")
+                nc.tensor.matmul(out=live["bias"][:], lhsT=ones[:], rhs=bias_row[:], start=True, stop=True)
+            elif tick == MEAN + 1:
+                nc.scalar.copy(out=bias_rows[:], in_=live["bias"][:])
+                nc.vector.tensor_copy(out=affine_rows_f32[:], in_=affine_rows[:])
+            elif tick == MEAN + 2:
+                live["affine"] = zt_psum.tile([P, P], F32, name="affine_ps", tag="z_turned")
+                nc.tensor.transpose(live["affine"][:], affine_rows_f32[:], ident[:])
+            elif tick == MEAN + 3:
+                affine = live["affine"][:, 0 : 2 * FEATURE_BLOCKS]
+                nc.scalar.mul(out=relu_cols[:], in_=affine, mul=1.0 - LEAKY_SLOPE)
+                nc.scalar.mul(out=line_cols[:], in_=affine, mul=LEAKY_SLOPE)
 
         def turn_h(x):
-            turned = turn_psum.tile([P, 2 * P], F32, name="turned")
+            if x < CELL_TILES + 1 and x % 3 < 2:
+                turned = back_psum.tile([P, 2 * P], F32, name="turned_early", tag="a_rows")
+            else:
+                turned = turn_psum.tile([P, 2 * P], F32, name="turned")
             live["turned", x] = turned
             pairs = rows_of(x).bitcast(F32)
             for u in range(2):
@@ -371,26 +385,20 @@ def tile_gnnnicheencoder_pa_t_kernel(
                 scale=1.0 / (D * D * D),
             )
 
-        def affine_term(pair, half, kind, on_vector):
-            if half == 0:
+        def affine_term(pair, half, jj, kind):
+            j = HALF_BLOCKS * half + jj
+            if j == 0:
                 live[kind, pair] = term_pool.tile([P, FEATURE_BLOCKS, PAIR, P], F32, name=kind)
             cols = relu_cols if kind == "relu_term" else line_cols
-            for jj in range(HALF_BLOCKS):
-                j = HALF_BLOCKS * half + jj
-                term = live[kind, pair][:, j, :, :].rearrange("p i r -> p (i r)")
-                z_block = live["z_turned", pair, half][:, jj, :, :].rearrange("p i r -> p (i r)")
-                gain = cols[:, j : j + 1]
-                shift = cols[:, FEATURE_BLOCKS + j : FEATURE_BLOCKS + j + 1]
-                if on_vector:
-                    nc.vector.tensor_scalar(out=term, in0=z_block, scalar1=gain, scalar2=shift, op0=ALU.mult, op1=ALU.add)
-                else:
-                    nc.scalar.activation(
-                        out=term,
-                        in_=z_block,
-                        func=ACT.Relu if kind == "relu_term" else ACT.Identity,
-                        bias=shift,
-                        scale=gain,
-                    )
+            term = live[kind, pair][:, j, :, :].rearrange("p i r -> p (i r)")
+            z_block = live["z_turned", pair, half][:, jj, :, :].rearrange("p i r -> p (i r)")
+            nc.scalar.activation(
+                out=term,
+                in_=z_block,
+                func=ACT.Relu if kind == "relu_term" else ACT.Identity,
+                bias=cols[:, FEATURE_BLOCKS + j : FEATURE_BLOCKS + j + 1],
+                scale=cols[:, j : j + 1],
+            )
 
         turning_order = {}
         for x in range(ROW_TILES):
@@ -439,16 +447,11 @@ def tile_gnnnicheencoder_pa_t_kernel(
             for_tile(quantise, tick, QUANTISE)
             for_tile(residual_and_store, tick, RESIDUAL)
             for_tile(average, tick, MEAN)
-            line_on_vector = tick > ROW_TILES - 1 + QUANTISE
-            if line_on_vector:
-                for_half_pair(lambda pair, half: affine_term(pair, half, "line_term", True), tick, AFFINE)
-            for_half_pair(lambda pair, half: affine_term(pair, half, "relu_term", False), tick, AFFINE)
-            if not line_on_vector:
-                for_half_pair(lambda pair, half: affine_term(pair, half, "line_term", False), tick, AFFINE)
+            for jj in range(HALF_BLOCKS):
+                for_half_pair(lambda pair, half: affine_term(pair, half, jj, "relu_term"), tick, AFFINE)
+                for_half_pair(lambda pair, half: affine_term(pair, half, jj, "line_term"), tick, AFFINE)
             for_tile(invert_std, tick, VARIANCE)
 
-        for tick in range(SUMS, MULTIPLY):
-            run_tick(tick)
-        prepare_affine_columns()
-        for tick in range(MULTIPLY, ROW_TILES + RESIDUAL):
+        for tick in range(SUMS, ROW_TILES + RESIDUAL):
+            prepare(tick)
             run_tick(tick)

from contextlib import ExitStack

import concourse.mybir as mybir
from concourse.masks import make_identity

F32 = mybir.dt.float32
BF16 = mybir.dt.bfloat16
I32 = mybir.dt.int32
U32 = mybir.dt.uint32
U8 = mybir.dt.uint8
FP8X4 = mybir.dt.float8_e4m3fn_x4
ALU = mybir.AluOpType
ACT = mybir.ActivationFunctionType

P = 128
PACK = 4
GRAPHS = 512
NODES = 17
D = 512
FEATURE_BLOCKS = D // P
ROWS = GRAPHS * NODES
ROW_TILES = ROWS // P
CELL_GRAPHS = 32
FOLD = P // CELL_GRAPHS
CELL_TILES = 4
CELLS = GRAPHS // CELL_GRAPHS
SPAN_CELLS = P // CELL_GRAPHS
SPAN_TILES = NODES
LAST = SPAN_TILES - 1
SPANS = ROW_TILES // SPAN_TILES
PAIR = 2
HALF_BLOCKS = FEATURE_BLOCKS // 2
LANE_HEAD = 3
LN_EPS = 1e-5
LEAKY_SLOPE = 0.01

LOAD = -10
TURN_H = -2
COPY_H = TURN_H + 1
MEAN = COPY_H + 1
QUANTISE = MEAN + 1
MULTIPLY = QUANTISE + 1
ADD_BIAS = MULTIPLY + 1
VARIANCE = ADD_BIAS + 1
NORMALISE = VARIANCE + 1
TURN_Z = NORMALISE + 1
AFFINE = TURN_Z + 1
TURN_BACK = AFFINE + 3
RESIDUAL = TURN_BACK + 1
SUMS = MEAN - CELL_TILES

FLOPS = 2 * 2 * ROWS * D * D


def load_weight(nc, pool, words_dram, scales_dram, label):
    words = pool.tile([P, D], U32, name=label + "_words", align_bytes=64)
    nc.sync.dma_start(
        out=words[:].bitcast(I32),
        in_=words_dram[0].rearrange("p n t -> p (n t)").bitcast(I32),
    )
    plane = pool.tile([P, D], U8, name=label + "_plane", align_bytes=64)
    nc.vector.memset(plane[:].bitcast(I32), 0)
    scale_rows = scales_dram[0].bitcast(I32)
    for quadrant in range(4):
        nc.sync.dma_start(
            out=plane[32 * quadrant : 32 * quadrant + 4, :].bitcast(I32),
            in_=scale_rows[4 * quadrant : 4 * quadrant + 4, :],
        )
    return words, plane


def cell_of(x):
    span, T = divmod(x, SPAN_TILES)
    return SPAN_CELLS * span + T // CELL_TILES, T % CELL_TILES


def is_last(x):
    return x % SPAN_TILES == LAST


def tile_gnnnicheencoder_pa_t_kernel(
    tc, h, W_l_words, W_l_scales, b_l, W_r_words, W_r_scales, ln_g, ln_b, out
):
    nc = tc.nc

    with ExitStack() as ctx:
        ctx.enter_context(tc.manual_schedule())
        consts = ctx.enter_context(tc.tile_pool(name="consts", bufs=1))
        cell_pool = ctx.enter_context(tc.tile_pool(name="cell_pool", bufs=8))
        last_pool = ctx.enter_context(tc.tile_pool(name="last_pool", bufs=4))
        pair_pool = ctx.enter_context(tc.tile_pool(name="pair_pool", bufs=6))
        last_pair_pool = ctx.enter_context(tc.tile_pool(name="last_pair_pool", bufs=2))
        code_pool = ctx.enter_context(tc.tile_pool(name="code_pool", bufs=4))
        c_pool = ctx.enter_context(tc.tile_pool(name="c_pool", bufs=5))
        work = ctx.enter_context(tc.tile_pool(name="work", bufs=4))
        z_pool = ctx.enter_context(tc.tile_pool(name="z_pool", bufs=6))
        term_pool = ctx.enter_context(tc.tile_pool(name="term_pool", bufs=3))
        stats = ctx.enter_context(tc.tile_pool(name="stats", bufs=6))
        turn_psum = ctx.enter_context(tc.psum_pool(name="turn_psum", bufs=1))
        acc_psum = ctx.enter_context(tc.psum_pool(name="acc_psum", bufs=1))
        sums_psum = ctx.enter_context(tc.psum_pool(name="sums_psum", bufs=2))
        zt_psum = ctx.enter_context(tc.psum_pool(name="zt_psum", bufs=2))
        back_psum = ctx.enter_context(tc.psum_pool(name="back_psum", bufs=2))

        cell_rows = {}
        last_rows = {}
        live = {}

        def rows_of(x):
            if is_last(x):
                return last_rows[x // SPAN_TILES][:]
            cell, j = cell_of(x)
            return cell_rows[cell][:, j, :]

        def load_last(span):
            last_rows[span] = last_pool.tile([P, D], BF16, name="last_rows")
            nc.sync.dma_start(out=last_rows[span][:], in_=h[P * span : P * (span + 1), NODES - 1, :])

        def load_cell(cell):
            cell_rows[cell] = cell_pool.tile([P, CELL_TILES, D], BF16, name="cell_rows")
            graphs = slice(CELL_GRAPHS * cell, CELL_GRAPHS * (cell + 1))
            for a in range(FOLD):
                nc.sync.dma_start(
                    out=cell_rows[cell][CELL_GRAPHS * a : CELL_GRAPHS * (a + 1), :, :],
                    in_=h[graphs, CELL_TILES * a : CELL_TILES * (a + 1), :],
                )

        eps_col = consts.tile([P, 1], F32, name="eps_col")
        nc.vector.memset(eps_col[:], LN_EPS)
        table_col = consts.tile([P, 1], F32, name="table_col")
        nc.scalar.activation(out=table_col[:], in_=eps_col[:], func=ACT.Abs_reciprocal_sqrt, bias=eps_col[:], scale=1.0)
        bias_row = consts.tile([P, D], BF16, name="bias_row")
        nc.vector.memset(bias_row[:], 0.0)
        nc.scalar.dma_start(out=bias_row[0:1, :], in_=b_l.rearrange("(o f) -> o f", o=1))
        affine_rows = consts.tile([P, P], BF16, name="affine_rows")
        nc.vector.memset(affine_rows[:], 0.0)
        nc.scalar.dma_start(out=affine_rows[0:FEATURE_BLOCKS, :], in_=ln_g.rearrange("(j p) -> j p", p=P))
        nc.scalar.dma_start(
            out=affine_rows[FEATURE_BLOCKS : 2 * FEATURE_BLOCKS, :], in_=ln_b.rearrange("(j p) -> j p", p=P)
        )
        load_last(0)
        load_cell(0)
        load_cell(1)
        wl_words, wl_plane = load_weight(nc, consts, W_l_words, W_l_scales, "wl")
        wr_words, wr_plane = load_weight(nc, consts, W_r_words, W_r_scales, "wr")
        load_cell(2)

        ident = consts.tile([P, P], F32, name="ident")
        make_identity(nc, ident[:])

        offset = consts.tile([P, SPAN_CELLS, CELL_GRAPHS], I32, name="offset")
        nc.gpsimd.iota(
            offset[:], pattern=[[-CELL_GRAPHS, SPAN_CELLS], [-1, CELL_GRAPHS]], base=0, channel_multiplier=1
        )
        pick = consts.tile([P, SPAN_CELLS, CELL_GRAPHS], BF16, name="pick")
        nc.vector.tensor_scalar(
            out=pick[:].rearrange("p q g -> p (q g)"),
            in0=offset[:].rearrange("p q g -> p (q g)"),
            scalar1=0.0,
            scalar2=1.0 / (NODES - 1),
            op0=ALU.is_equal,
            op1=ALU.mult,
        )
        fold = consts.tile([P, CELL_GRAPHS], BF16, name="fold")
        offset_in_cell = consts.tile([P, CELL_GRAPHS], I32, name="offset_in_cell")
        nc.vector.tensor_single_scalar(
            out=offset_in_cell[:], in_=offset[:, 0, :], scalar=CELL_GRAPHS - 1, op=ALU.bitwise_and
        )
        nc.vector.tensor_scalar(
            out=fold[:],
            in0=offset_in_cell[:],
            scalar1=0.0,
            scalar2=1.0 / (NODES - 1),
            op0=ALU.is_equal,
            op1=ALU.mult,
        )

        ones = consts.tile([P, P], BF16, name="ones")
        nc.vector.memset(ones[:], 1.0)
        bias_rows = consts.tile([P, D], BF16, name="bias_rows")

        relu_cols = consts.tile([P, 2 * FEATURE_BLOCKS], F32, name="relu_cols")
        line_cols = consts.tile([P, 2 * FEATURE_BLOCKS], F32, name="line_cols")

        affine_rows_f32 = consts.tile([P, P], F32, name="affine_rows_f32")

        def prepare(tick):
            if tick == MEAN:
                live["bias"] = zt_psum.tile([P, D], F32, name="bias_ps", tag="z_turned")
                nc.tensor.matmul(out=live["bias"][:], lhsT=ones[:], rhs=bias_row[:], start=True, stop=True)
            elif tick == MEAN + 1:
                nc.scalar.copy(out=bias_rows[:], in_=live["bias"][:])
                nc.vector.tensor_copy(out=affine_rows_f32[:], in_=affine_rows[:])
            elif tick == MEAN + 2:
                live["affine"] = zt_psum.tile([P, P], F32, name="affine_ps", tag="z_turned")
                nc.tensor.transpose(live["affine"][:], affine_rows_f32[:], ident[:])
            elif tick == MEAN + 3:
                affine = live["affine"][:, 0 : 2 * FEATURE_BLOCKS]
                nc.scalar.mul(out=relu_cols[:], in_=affine, mul=1.0 - LEAKY_SLOPE)
                nc.scalar.mul(out=line_cols[:], in_=affine, mul=LEAKY_SLOPE)

        def turn_h(x):
            if x < CELL_TILES + 1 and x % 3 < 2:
                turned = back_psum.tile([P, 2 * P], F32, name="turned_early", tag="a_rows")
            else:
                turned = turn_psum.tile([P, 2 * P], F32, name="turned")
            live["turned", x] = turned
            pairs = rows_of(x).bitcast(F32)
            for u in range(2):
                nc.tensor.transpose(turned[:, P * u : P * (u + 1)], pairs[:, u : D // 2 : 2], ident[:])

        def sum_lane(cell, t, first_part, end_part):
            if t == 0 and first_part == 0:
                live["sums", cell] = sums_psum.tile([P, CELL_GRAPHS, PACK], F32, name="sums")
            span, q = divmod(cell, SPAN_CELLS)
            for i in range(first_part, end_part):
                rows = cell_rows[cell][:, i, :] if i < CELL_TILES else last_rows[span][:]
                nc.tensor.matmul(
                    out=live["sums", cell][:, :, t],
                    lhsT=rows[:, t:D:PACK],
                    rhs=fold[:] if i < CELL_TILES else pick[:, q, :],
                    start=(i == 0),
                    stop=(i == CELL_TILES),
                )

        def multiply(x):
            acc = acc_psum.tile([P, D], F32, name="acc")
            live["acc", x] = acc
            words, plane = live["codes", x]
            for operand, w_words, w_plane in ((1, wl_words, wl_plane), (0, wr_words, wr_plane)):
                cols = slice(P * operand, P * (operand + 1))
                nc.tensor.matmul_mx(
                    out=acc[:],
                    lhsT=words[:, cols].bitcast(FP8X4),
                    lhsT_scale=plane[:, cols],
                    rhs=w_words[:].bitcast(FP8X4),
                    rhs_scale=w_plane[:],
                    start=(operand == 1),
                    stop=(operand == 0),
                )

        def turn_z(pair, half):
            z_turned = zt_psum.tile([P, HALF_BLOCKS, PAIR, P], F32, name="z_turned")
            live["z_turned", pair, half] = z_turned
            for jj in range(HALF_BLOCKS):
                j = HALF_BLOCKS * half + jj
                for i in range(PAIR):
                    nc.tensor.transpose(
                        z_turned[:, jj, i, :], live["z", PAIR * pair + i][:, P * j : P * (j + 1)], ident[:]
                    )

        def turn_back(x):
            a_rows = back_psum.tile([P, D], F32, name="a_rows")
            live["a_rows", x] = a_rows
            pair, i = divmod(x, PAIR)
            for j in range(FEATURE_BLOCKS):
                block = a_rows[:, P * j : P * (j + 1)]
                nc.tensor.matmul(
                    out=block,
                    lhsT=live["relu_term", pair][:, j, i, :],
                    rhs=ident[:],
                    is_transpose=True,
                    start=True,
                    stop=False,
                )
                nc.tensor.matmul(
                    out=block,
                    lhsT=live["line_term", pair][:, j, i, :],
                    rhs=ident[:],
                    is_transpose=True,
                    start=False,
                    stop=True,
                )

        def average_part(pair_tile, rows, cell, times):
            shape = [P, times, CELL_GRAPHS * PACK]
            nc.vector.scalar_tensor_tensor(
                out=pair_tile[:, 1, rows, :].rearrange("p (a g) t -> p a (g t)", a=times),
                in0=pair_tile[:, 0, rows, :].rearrange("p (a g) t -> p a (g t)", a=times),
                scalar=-1.0 / (NODES - 1),
                in1=live["sums", cell][:].rearrange("p g t -> p (g t)").unsqueeze(1).to_broadcast(shape),
                op0=ALU.mult,
                op1=ALU.add,
            )

        def average(x):
            if is_last(x):
                return
            cell, j = cell_of(x)
            average_part(live["hm", x], slice(0, P), cell, FOLD)
            if j == CELL_TILES - 1:
                span, q = divmod(cell, SPAN_CELLS)
                rows = slice(CELL_GRAPHS * q, CELL_GRAPHS * (q + 1))
                average_part(live["hm", SPAN_TILES * span + LAST], rows, cell, 1)

        def quantise(x):
            words = code_pool.tile([P, 2 * P], U32, name="words", align_bytes=64)
            plane = code_pool.tile([P, 2 * P], U8, name="plane", align_bytes=64)
            live["codes", x] = words, plane
            nc.vector.quantize_mx(
                out=words[:].bitcast(FP8X4),
                scales=plane[:],
                in_=live["hm", x][:].rearrange("p o r t -> p (o r t)"),
            )

        def add_bias(x):
            c = c_pool.tile([P, D], F32, name="c")
            row_sum = stats.tile([P, 1], F32, name="row_sum")
            live["c", x] = c
            live["row_sum", x] = row_sum
            nc.vector.scalar_tensor_tensor(
                out=c[:],
                in0=live["acc", x][:],
                scalar=1.0,
                in1=bias_rows[:],
                op0=ALU.mult,
                op1=ALU.add,
                accum_out=row_sum[:],
            )

        def residual_and_store(x):
            result = work.tile([P, D], F32, name="result")
            nc.vector.tensor_tensor(out=result[:], in0=live["a_rows", x][:], in1=rows_of(x), op=ALU.add)
            if is_last(x):
                span = x // SPAN_TILES
                nc.sync.dma_start(out=out[P * span : P * (span + 1), NODES - 1, :], in_=result[:])
            else:
                cell, j = cell_of(x)
                graphs = slice(CELL_GRAPHS * cell, CELL_GRAPHS * (cell + 1))
                for a in range(FOLD):
                    nc.sync.dma_start(
                        out=out[graphs, CELL_TILES * a + j, :],
                        in_=result[CELL_GRAPHS * a : CELL_GRAPHS * (a + 1), :],
                    )

        def negate_mean(x):
            neg_mean = stats.tile([P, 1], F32, name="neg_mean")
            live["neg_mean", x] = neg_mean
            nc.gpsimd.tensor_scalar(
                out=neg_mean[:], in0=live["row_sum", x][:], scalar1=-1.0 / D, scalar2=0.0, op0=ALU.mult, op1=ALU.add
            )

        def normalise(x):
            z = z_pool.tile([P, D], F32, name="z")
            live["z", x] = z
            nc.gpsimd.tensor_scalar(
                out=z[:],
                in0=live["c", x][:],
                scalar1=live["neg_mean", x][:],
                scalar2=live["rstd", x][:],
                op0=ALU.add,
                op1=ALU.mult,
            )

        def copy_h(x):
            pool = last_pair_pool if is_last(x) else pair_pool
            hm = pool.tile([P, 2, P, PACK], BF16, name="hm", align_bytes=64)
            live["hm", x] = hm
            nc.scalar.copy(
                out=hm[:, 0, :, :].rearrange("p r t -> p (r t)").bitcast(F32).rearrange("p (r u) -> p r u", u=2),
                in_=live["turned", x][:].rearrange("p (u r) -> p r u", u=2),
            )

        def sum_squares(x):
            squares = work.tile([P, D], F32, name="squares")
            sq_sum = stats.tile([P, 1], F32, name="sq_sum")
            live["sq_sum", x] = sq_sum
            nc.scalar.activation(
                out=squares[:],
                in_=live["c", x][:],
                func=ACT.Square,
                bias=live["row_sum", x][:],
                scale=-float(D),
                accum_out=sq_sum[:],
            )

        def invert_std(x):
            rstd = stats.tile([P, 1], F32, name="rstd")
            live["rstd", x] = rstd
            nc.scalar.activation(
                out=rstd[:],
                in_=live["sq_sum", x][:],
                func=ACT.Abs_reciprocal_sqrt,
                bias=eps_col[:],
                scale=1.0 / (D * D * D),
            )

        def affine_term(pair, half, jj, kind):
            j = HALF_BLOCKS * half + jj
            if j == 0:
                live[kind, pair] = term_pool.tile([P, FEATURE_BLOCKS, PAIR, P], F32, name=kind)
            cols = relu_cols if kind == "relu_term" else line_cols
            term = live[kind, pair][:, j, :, :].rearrange("p i r -> p (i r)")
            z_block = live["z_turned", pair, half][:, jj, :, :].rearrange("p i r -> p (i r)")
            nc.scalar.activation(
                out=term,
                in_=z_block,
                func=ACT.Relu if kind == "relu_term" else ACT.Identity,
                bias=cols[:, FEATURE_BLOCKS + j : FEATURE_BLOCKS + j + 1],
                scale=cols[:, j : j + 1],
            )

        turning_order = {}
        for x in range(ROW_TILES):
            turning_order[x if not is_last(x) else x - SPAN_TILES] = x
        first_tile = {SPAN_TILES * (cell // SPAN_CELLS) + CELL_TILES * (cell % SPAN_CELLS): cell for cell in range(CELLS)}

        def for_tile(step, tick, lag):
            if 0 <= tick - lag < ROW_TILES:
                step(tick - lag)

        def for_turning(step, tick, lag):
            if tick - lag in turning_order:
                step(turning_order[tick - lag])

        def for_half_pair(step, tick, lag):
            pair, half = divmod(tick - lag - (PAIR - 1), PAIR)
            if 0 <= pair < ROW_TILES // PAIR:
                step(pair, half)

        def for_lane(tick, first_part, end_part):
            for t in range(PACK):
                cell = first_tile.get(tick - SUMS - t)
                if cell is not None:
                    sum_lane(cell, t, first_part, end_part)

        def load(tick):
            cell = first_tile.get(tick - LOAD)
            if cell is not None and cell > 2:
                if cell % SPAN_CELLS == 0:
                    load_last(cell // SPAN_CELLS)
                load_cell(cell)

        def run_tick(tick):
            load(tick)
            for_turning(copy_h, tick, COPY_H)
            for_tile(sum_squares, tick, VARIANCE)
            for_tile(add_bias, tick, ADD_BIAS)
            for_half_pair(turn_z, tick, TURN_Z)
            for_tile(turn_back, tick, TURN_BACK)
            for_turning(turn_h, tick, TURN_H)
            for_lane(tick, 0, LANE_HEAD)
            for_tile(multiply, tick, MULTIPLY)
            for_lane(tick, LANE_HEAD, CELL_TILES + 1)
            for_tile(normalise, tick, NORMALISE)
            for_tile(negate_mean, tick, VARIANCE)
            for_tile(quantise, tick, QUANTISE)
            for_tile(residual_and_store, tick, RESIDUAL)
            for_tile(average, tick, MEAN)
            for jj in range(HALF_BLOCKS):
                for_half_pair(lambda pair, half: affine_term(pair, half, jj, "relu_term"), tick, AFFINE)
                for_half_pair(lambda pair, half: affine_term(pair, half, jj, "line_term"), tick, AFFINE)
            for_tile(invert_std, tick, VARIANCE)

        for tick in range(SUMS, ROW_TILES + RESIDUAL):
            prepare(tick)
            run_tick(tick)
